import numpy as np
import ml_dtypes


def mxq(x, axis, fmt="e4m3"):
    dtype, down = {"e4m3": (ml_dtypes.float8_e4m3fn, 7), "e5m2": (ml_dtypes.float8_e5m2, 14)}[fmt]
    v = np.moveaxis(np.asarray(x, np.float32).astype(ml_dtypes.bfloat16).astype(np.float64), axis, -1)
    blocks = v.reshape(v.shape[:-1] + (-1, 32))
    amax = np.abs(blocks).max(-1, keepdims=True)
    byte = np.maximum(np.where(amax > 0, np.frexp(amax)[1] - 1 + 127, 0) - down, 1)
    scale = np.exp2(byte - 127.0)
    codes = (blocks / scale).astype(np.float32).astype(dtype).astype(np.float64)
    return np.moveaxis((codes * scale).reshape(v.shape), -1, axis)


WIDE = False


def mx_kscale(k):
    if not WIDE:
        return np.ones(k)
    levels = np.array([10, -10, 5, -5, 0])
    if k % 512:
        return np.exp2(np.random.permutation(np.resize(levels, k // 32))).repeat(32)
    a = np.empty((k // 512, 16))
    for p in range(k // 512):
        a[p, :8] = np.random.permutation(np.resize(levels, 8))
        for g in range(8):
            far = levels[np.abs(levels - a[p, g]) >= 10]
            a[p, g + 8] = far[np.random.randint(len(far))]
    return np.exp2(a.ravel()).repeat(32)


BF16 = ml_dtypes.bfloat16


def bf(x):
    return np.asarray(x, np.float32).astype(BF16)


def f64(x):
    return np.asarray(x).astype(np.float64)


B, L, D, F, K = 256, 8, 512, 1024, 16
EPS = 1e-12


def silu(v):
    return v / (1.0 + np.exp(-v))


def l2norm(t, axis):
    n = np.sqrt((t * t).sum(axis=axis, keepdims=True))
    return t / np.maximum(n, EPS)


def mix_draw(rows, cols):
    return np.random.standard_normal((L, rows, cols)) * np.sqrt(np.e / K) * np.exp(0.5 * np.random.standard_normal((L, 1, cols)))


def hidden_draw():
    return silu(3.0 * np.random.standard_normal((B, L, F))) * np.random.standard_normal((B, L, F)) * 3.0 / np.sqrt(D)


def setup_inputs():
    t = mx_kscale(F)
    g = np.sqrt(np.mean(1.0 / t**2))
    return {"h": bf(hidden_draw() * t * g),
            "w_down_mix": bf(mix_draw(F, D) / t[:, None])}


def reference(h, w_down_mix):
    wd = l2norm(f64(w_down_mix), 1)
    y = mxq(f64(h).transpose(1, 0, 2), 2, "e4m3") @ mxq(wd, 1, "e4m3")
    return l2norm(y, -1).transpose(1, 0, 2)

@@ -1,0 +1,192 @@
+from contextlib import ExitStack
+
+import concourse.mybir as mybir
+from concourse.masks import make_identity
+
+BF16 = mybir.dt.bfloat16
+F32 = mybir.dt.float32
+U32 = mybir.dt.uint32
+U8 = mybir.dt.uint8
+FP8X4 = mybir.dt.float8_e4m3fn_x4
+ACT = mybir.ActivationFunctionType
+ALU = mybir.AluOpType
+
+P = 128
+PACK = 4
+BATCH, TOKENS, HIDDEN, OUT = 256, 8, 1024, 512
+PASSES = HIDDEN // (P * PACK)
+ROWS = PASSES * PACK
+HALVES = 2
+B_TILES = BATCH // P
+J_BLOCKS = OUT // P
+EPS = 1e-12
+TOKENS_PER_H_LOAD = 2
+VECTOR_COLS = 320
+RUN = 4
+
+FLOPS = 2 * BATCH * TOKENS * HIDDEN * OUT
+
+
+def tile_npertokenswishglu_basis_pb_kernel(tc, h, w_down_mix, out):
+    nc = tc.nc
+    with ExitStack() as stack:
+        const = stack.enter_context(tc.tile_pool(name="const", bufs=1))
+        w_pool = stack.enter_context(tc.tile_pool(name="w_pool", bufs=TOKENS))
+        h_pool = stack.enter_context(tc.tile_pool(name="h_pool", bufs=TOKENS // TOKENS_PER_H_LOAD))
+        h_mx = stack.enter_context(tc.tile_pool(name="h_mx", bufs=TOKENS))
+        work = stack.enter_context(tc.tile_pool(name="work", bufs=2))
+        unread = stack.enter_context(tc.tile_pool(name="unread", bufs=4))
+        small = stack.enter_context(tc.tile_pool(name="small", bufs=4))
+        result = stack.enter_context(tc.tile_pool(name="result", bufs=3))
+        wT_psum = stack.enter_context(tc.psum_pool(name="wT_psum", bufs=3))
+        inv_psum = stack.enter_context(tc.psum_pool(name="inv_psum", bufs=2))
+        hT_psum = stack.enter_context(tc.psum_pool(name="hT_psum", bufs=1))
+        y_psum = stack.enter_context(tc.psum_pool(name="y_psum", bufs=2))
+
+        w_sb = []
+        h_sb = []
+        h_view = h.rearrange("(i p) l f -> p i l f", p=P)
+        for l in range(TOKENS):
+            w_tile = w_pool.tile([P, ROWS, OUT], BF16, name="w_tile")
+            nc.sync.dma_start(
+                out=w_tile[:].rearrange("p (c t) j -> p c (t j)", t=PACK),
+                in_=w_down_mix[l].rearrange("(c p t) j -> p c (t j)", p=P, t=PACK),
+            )
+            w_sb.append(w_tile)
+            if l < TOKENS // TOKENS_PER_H_LOAD:
+                h_tile = h_pool.tile([P, B_TILES, TOKENS_PER_H_LOAD, HIDDEN], BF16, name="h_tile")
+                first = l * TOKENS_PER_H_LOAD
+                nc.sync.dma_start(out=h_tile[:], in_=h_view[:, :, first : first + TOKENS_PER_H_LOAD, :])
+                h_sb.append(h_tile)
+
+        ident_bf = const.tile([P, P], BF16, name="ident_bf")
+        make_identity(nc, ident_bf[:])
+        ident_f32 = const.tile([P, P], F32, name="ident_f32")
+        make_identity(nc, ident_f32[:])
+
+        one = const.tile([P, 1], F32, name="one")
+        nc.vector.memset(one[:], 1.0)
+        nc.scalar.activation(out=one[:], in_=one[:], func=ACT.Abs_reciprocal_sqrt)
+
+        def inverse_norm(sum_sq, width, name):
+            excess = small.tile([P, width], F32, name=name + "_excess")
+            nc.scalar.activation(out=excess[:], in_=sum_sq[:], func=ACT.Relu, bias=-EPS * EPS)
+            inv = small.tile([P, width], F32, name=name + "_inv")
+            nc.scalar.activation(out=inv[:], in_=excess[:], func=ACT.Abs_reciprocal_sqrt, bias=EPS * EPS)
+            return inv
+
+        def weight_norms(l):
+            col_sq = small.tile([P, J_BLOCKS], F32, name="col_sq")
+            for m in range(J_BLOCKS):
+                wT = wT_psum.tile([P, ROWS, P], BF16, name="wT")
+                for r in range(ROWS):
+                    nc.tensor.transpose(wT[:, r, :], w_sb[l][:, r, m * P : (m + 1) * P], ident_bf[:])
+                squares = unread.tile([P, ROWS * P], BF16, name="squares")
+                nc.scalar.activation(
+                    out=squares[:],
+                    in_=wT[:].rearrange("p r f -> p (r f)"),
+                    func=ACT.Square,
+                    accum_out=col_sq[:, m : m + 1],
+                )
+            col_inv = inverse_norm(col_sq, J_BLOCKS, "col")
+            inv_rows = inv_psum.tile([P, OUT], F32, name="inv_rows")
+            for m in range(J_BLOCKS):
+                nc.tensor.matmul(
+                    out=inv_rows[:, m * P : (m + 1) * P],
+                    lhsT=col_inv[:, m : m + 1].to_broadcast([P, P]),
+                    rhs=ident_f32[:],
+                    start=True,
+                    stop=True,
+                )
+            return inv_rows
+
+        def scale_columns(engine, l, c, first, last, inv, nd):
+            engine.tensor_tensor(
+                out=nd[:, c, first:last, :].rearrange("p (n i) t -> p n t i", i=RUN),
+                in0=w_sb[l][:, c * PACK : (c + 1) * PACK, first:last].rearrange("p t (n i) -> p n t i", i=RUN),
+                in1=inv.rearrange("p (n i) -> p n i", i=RUN)
+                .unsqueeze(2)
+                .to_broadcast([P, (last - first) // RUN, PACK, RUN]),
+                op=ALU.mult,
+            )
+
+        def quantise_weight(l, inv_rows):
+            nd = work.tile([P, PASSES, OUT, PACK], BF16, name="nd", align_bytes=64)
+            codes = work.tile([P, PASSES, OUT], U32, name="w_codes", align_bytes=64)
+            scales = work.tile([P, PASSES, OUT], U8, name="w_scales", align_bytes=64)
+            inv_gpsimd = work.tile([P, OUT - VECTOR_COLS], F32, name="inv_gpsimd")
+            nc.vector.tensor_copy(out=inv_gpsimd[:], in_=inv_rows[:, VECTOR_COLS:])
+            for c in range(PASSES):
+                scale_columns(nc.gpsimd, l, c, VECTOR_COLS, OUT, inv_gpsimd[:], nd)
+                scale_columns(nc.vector, l, c, 0, VECTOR_COLS, inv_rows[:, :VECTOR_COLS], nd)
+            for c in range(PASSES):
+                nc.vector.quantize_mx(
+                    out=codes[:, c, :].bitcast(FP8X4),
+                    scales=scales[:, c, :],
+                    in_=nd[:, c].rearrange("p j t -> p (j t)"),
+                )
+            return codes, scales
+
+        def quantise_hidden(l):
+            h_tile = h_sb[l // TOKENS_PER_H_LOAD]
+            grouped = work.tile([P, PASSES * BATCH * PACK], BF16, name="h_grouped", align_bytes=64)
+            grouped_words = grouped[:].bitcast(F32).rearrange("p (c b u) -> p c b u", c=PASSES, u=HALVES)
+            for c in range(PASSES):
+                hT = hT_psum.tile([P, HALVES, B_TILES, P], F32, name="hT")
+                for u in range(HALVES):
+                    for i in range(B_TILES):
+                        words = h_tile[:, i, l % TOKENS_PER_H_LOAD, :].bitcast(F32)
+                        first = c * HALVES * P
+                        nc.tensor.transpose(
+                            hT[:, u, i, :], words[:, first + u : first + HALVES * P : HALVES], ident_f32[:]
+                        )
+                nc.vector.tensor_copy(out=grouped_words[:, c], in_=hT[:].rearrange("p u i b -> p (i b) u"))
+            codes = h_mx.tile([P, PASSES * BATCH], U32, name="h_codes", align_bytes=64)
+            scales = h_mx.tile([P, PASSES * BATCH], U8, name="h_scales", align_bytes=64)
+            nc.vector.quantize_mx(out=codes[:].bitcast(FP8X4), scales=scales[:], in_=grouped[:])
+            return codes, scales
+
+        def project(l, h_q, w_q):
+            h_codes, h_scales = h_q
+            w_codes, w_scales = w_q
+            row_sq = small.tile([P, B_TILES], F32, name="row_sq")
+            y_tiles = []
+            for i in range(B_TILES):
+                y = y_psum.tile([P, OUT], F32, name="y")
+                for c in range(PASSES):
+                    b_cols = slice((c * B_TILES + i) * P, (c * B_TILES + i + 1) * P)
+                    nc.tensor.matmul_mx(
+                        out=y[:],
+                        lhsT=h_codes[:, b_cols].bitcast(FP8X4),
+                        lhsT_scale=h_scales[:, b_cols],
+                        rhs=w_codes[:, c, :].bitcast(FP8X4),
+                        rhs_scale=w_scales[:, c, :],
+                        start=(c == 0),
+                        stop=(c == PASSES - 1),
+                    )
+                y_squares = unread.tile([P, OUT], BF16, name="y_squares")
+                nc.scalar.activation(
+                    out=y_squares[:], in_=y[:], func=ACT.Square, accum_out=row_sq[:, i : i + 1]
+                )
+                y_tiles.append(y)
+            row_inv = inverse_norm(row_sq, B_TILES, "row")
+            unit = result.tile([P, B_TILES, OUT], F32, name="unit")
+            nc.scalar.activation(out=unit[:, 0, :], in_=y_tiles[0][:], func=ACT.Copy, scale=row_inv[:, 0:1])
+            nc.vector.tensor_scalar_mul(out=unit[:, 1, :], in0=y_tiles[1][:], scalar1=row_inv[:, 1:2])
+            nc.sync.dma_start(out=out.rearrange("(i p) l j -> p i l j", p=P)[:, :, l, :], in_=unit[:])
+
+        NORMS_AHEAD = 1
+        HIDDEN_AHEAD = 2
+        inv_rows = {}
+        h_q = {}
+        for l in range(NORMS_AHEAD):
+            inv_rows[l] = weight_norms(l)
+        for l in range(HIDDEN_AHEAD):
+            h_q[l] = quantise_hidden(l)
+        for l in range(TOKENS):
+            if l + NORMS_AHEAD < TOKENS:
+                inv_rows[l + NORMS_AHEAD] = weight_norms(l + NORMS_AHEAD)
+            if l + HIDDEN_AHEAD < TOKENS:
+                h_q[l + HIDDEN_AHEAD] = quantise_hidden(l + HIDDEN_AHEAD)
+            w_q = quantise_weight(l, inv_rows[l])
+            project(l, h_q[l], w_q)

@@ -20,10 +20,13 @@ HALVES = 2
 B_TILES = BATCH // P
 J_BLOCKS = OUT // P
 EPS = 1e-12
-TOKENS_PER_H_LOAD = 2
-VECTOR_COLS = 320
+GRAM_TOKENS = 2
+VECTOR_COLS = 304
 RUN = 4
 
+SCALAR_UNIT = (4, 4)
+SCALAR_HIDDEN = 6
+SCALAR_SHARE = (0,)
 FLOPS = 2 * BATCH * TOKENS * HIDDEN * OUT
 
 
@@ -32,77 +35,132 @@ def tile_npertokenswishglu_basis_pb_kernel(tc, h, w_down_mix, out):
     with ExitStack() as stack:
         const = stack.enter_context(tc.tile_pool(name="const", bufs=1))
         w_pool = stack.enter_context(tc.tile_pool(name="w_pool", bufs=TOKENS))
-        h_pool = stack.enter_context(tc.tile_pool(name="h_pool", bufs=TOKENS // TOKENS_PER_H_LOAD))
-        h_mx = stack.enter_context(tc.tile_pool(name="h_mx", bufs=TOKENS))
+        h_pool = stack.enter_context(tc.tile_pool(name="h_pool", bufs=TOKENS))
         work = stack.enter_context(tc.tile_pool(name="work", bufs=2))
-        unread = stack.enter_context(tc.tile_pool(name="unread", bufs=4))
-        small = stack.enter_context(tc.tile_pool(name="small", bufs=4))
+        unread = stack.enter_context(tc.tile_pool(name="unread", bufs=2))
+        small = stack.enter_context(tc.tile_pool(name="small", bufs=TOKENS))
         result = stack.enter_context(tc.tile_pool(name="result", bufs=3))
-        wT_psum = stack.enter_context(tc.psum_pool(name="wT_psum", bufs=3))
-        inv_psum = stack.enter_context(tc.psum_pool(name="inv_psum", bufs=2))
-        hT_psum = stack.enter_context(tc.psum_pool(name="hT_psum", bufs=1))
-        y_psum = stack.enter_context(tc.psum_pool(name="y_psum", bufs=2))
+        wT_psum = stack.enter_context(tc.psum_pool(name="wT_psum", bufs=2))
+        inv_psum = stack.enter_context(tc.psum_pool(name="inv_psum", bufs=1))
+        hT_psum = stack.enter_context(tc.psum_pool(name="hT_psum", bufs=2))
+        y_psum = stack.enter_context(tc.psum_pool(name="y_psum", bufs=3))
+        stack.enter_context(tc.manual_schedule())
 
-        w_sb = []
-        h_sb = []
-        h_view = h.rearrange("(i p) l f -> p i l f", p=P)
-        for l in range(TOKENS):
-            w_tile = w_pool.tile([P, ROWS, OUT], BF16, name="w_tile")
-            nc.sync.dma_start(
-                out=w_tile[:].rearrange("p (c t) j -> p c (t j)", t=PACK),
-                in_=w_down_mix[l].rearrange("(c p t) j -> p c (t j)", p=P, t=PACK),
-            )
-            w_sb.append(w_tile)
-            if l < TOKENS // TOKENS_PER_H_LOAD:
-                h_tile = h_pool.tile([P, B_TILES, TOKENS_PER_H_LOAD, HIDDEN], BF16, name="h_tile")
-                first = l * TOKENS_PER_H_LOAD
-                nc.sync.dma_start(out=h_tile[:], in_=h_view[:, :, first : first + TOKENS_PER_H_LOAD, :])
-                h_sb.append(h_tile)
-
-        ident_bf = const.tile([P, P], BF16, name="ident_bf")
-        make_identity(nc, ident_bf[:])
         ident_f32 = const.tile([P, P], F32, name="ident_f32")
         make_identity(nc, ident_f32[:])
+        ident_bf = const.tile([P, P], BF16, name="ident_bf")
+        make_identity(nc, ident_bf[:])
 
         one = const.tile([P, 1], F32, name="one")
         nc.vector.memset(one[:], 1.0)
         nc.scalar.activation(out=one[:], in_=one[:], func=ACT.Abs_reciprocal_sqrt)
 
-        def inverse_norm(sum_sq, width, name):
-            excess = small.tile([P, width], F32, name=name + "_excess")
+        w_sb = {}
+        h_sb = {}
+        h_view = h.rearrange("(i p) l f -> p i l f", p=P)
+
+        def load_weight(l, loads):
+            w_sb[l] = w_pool.tile([P, ROWS, OUT], BF16, name="w_tile")
+            w_out = w_sb[l][:].rearrange("p (c t) j -> p c (t j)", t=PACK)
+            w_in = w_down_mix[l].rearrange("(c p t) j -> p c (t j)", p=P, t=PACK)
+            step = PASSES // loads
+            for c in range(0, PASSES, step):
+                nc.sync.dma_start(out=w_out[:, c : c + step], in_=w_in[:, c : c + step])
+
+        def load_hidden(l):
+            h_sb[l] = h_pool.tile([P, B_TILES, HIDDEN], BF16, name="h_tile")
+            nc.sync.dma_start(out=h_sb[l][:], in_=h_view[:, :, l, :])
+
+        WEIGHTS_FIRST = 2
+        for l in range(TOKENS + WEIGHTS_FIRST - 1):
+            if l < TOKENS:
+                load_weight(l, PASSES if l == 0 else 1)
+            if l >= WEIGHTS_FIRST - 1:
+                load_hidden(l - WEIGHTS_FIRST + 1)
+
+        wT = {}
+        col_sq = {}
+        col_inv = {}
+        inv_rows = {}
+        inv_gpsimd = {}
+        nd = {}
+        w_codes = {}
+        w_scales = {}
+        grouped = {}
+        hT = {}
+        h_codes = {}
+        h_scales = {}
+        y = {}
+        row_sq = {}
+        row_inv = {}
+        unit = {}
+        gram = {}
+
+        def clamp(sum_sq, name):
+            excess = small.tile([P, sum_sq.shape[1]], F32, name=name + "_excess")
             nc.scalar.activation(out=excess[:], in_=sum_sq[:], func=ACT.Relu, bias=-EPS * EPS)
-            inv = small.tile([P, width], F32, name=name + "_inv")
+            return excess
+
+        def invert(excess, name):
+            inv = small.tile([P, excess.shape[1]], F32, name=name + "_inv")
             nc.scalar.activation(out=inv[:], in_=excess[:], func=ACT.Abs_reciprocal_sqrt, bias=EPS * EPS)
             return inv
 
-        def weight_norms(l):
-            col_sq = small.tile([P, J_BLOCKS], F32, name="col_sq")
-            for m in range(J_BLOCKS):
-                wT = wT_psum.tile([P, ROWS, P], BF16, name="wT")
-                for r in range(ROWS):
-                    nc.tensor.transpose(wT[:, r, :], w_sb[l][:, r, m * P : (m + 1) * P], ident_bf[:])
-                squares = unread.tile([P, ROWS * P], BF16, name="squares")
-                nc.scalar.activation(
-                    out=squares[:],
-                    in_=wT[:].rearrange("p r f -> p (r f)"),
-                    func=ACT.Square,
-                    accum_out=col_sq[:, m : m + 1],
-                )
-            col_inv = inverse_norm(col_sq, J_BLOCKS, "col")
-            inv_rows = inv_psum.tile([P, OUT], F32, name="inv_rows")
-            for m in range(J_BLOCKS):
-                nc.tensor.matmul(
-                    out=inv_rows[:, m * P : (m + 1) * P],
-                    lhsT=col_inv[:, m : m + 1].to_broadcast([P, P]),
-                    rhs=ident_f32[:],
-                    start=True,
-                    stop=True,
-                )
-            return inv_rows
+        def turn_weight(l, m, passes=range(PASSES)):
+            if passes[0] == 0:
+                wT[l, m] = wT_psum.tile([P, ROWS, P], BF16, name="wT")
+            for r in range(passes[0] * PACK, (passes[-1] + 1) * PACK):
+                nc.tensor.transpose(wT[l, m][:, r, :], w_sb[l][:, r, m * P : (m + 1) * P], ident_bf[:])
 
-        def scale_columns(engine, l, c, first, last, inv, nd):
+        def column_squares(l, m):
+            if l not in col_sq:
+                col_sq[l] = small.tile([P, J_BLOCKS], F32, name="col_sq")
+            squares = unread.tile([P, ROWS * P], BF16, name="squares")
+            nc.scalar.activation(
+                out=squares[:],
+                in_=wT[l, m][:].rearrange("p r f -> p (r f)"),
+                func=ACT.Square,
+                accum_out=col_sq[l][:, m : m + 1],
+            )
+
+        def gram_products(l, m, c):
+            if c == 0:
+                gram[l, m] = y_psum.tile([P, OUT], F32, name="y")
+            for r in range(c * PACK, (c + 1) * PACK):
+                block = w_sb[l][:, r, m * P : (m + 1) * P]
+                nc.tensor.matmul(
+                    out=gram[l, m][:, :P], lhsT=block, rhs=block, start=(r == 0), stop=(r == ROWS - 1)
+                )
+
+        def gram_diagonal(l, m):
+            diagonal = unread.tile([P, P], F32, name="diagonal")
+            nc.vector.scalar_tensor_tensor(
+                out=diagonal[:],
+                in0=gram[l, m][:, :P],
+                scalar=1.0,
+                in1=ident_f32[:],
+                op0=ALU.mult,
+                op1=ALU.mult,
+                accum_out=col_sq[l][:, m : m + 1],
+            )
+
+        def spread_norms(l):
+            inv_rows[l] = inv_psum.tile([P, OUT], F32, name="inv_rows")
+            for m in range(J_BLOCKS):
+                nc.tensor.transpose(
+                    inv_rows[l][:, m * P : (m + 1) * P],
+                    col_inv[l][:, m : m + 1].to_broadcast([P, P]),
+                    ident_f32[:],
+                )
+
+        def share_norms(l):
+            inv_gpsimd[l] = work.tile([P, OUT - VECTOR_COLS], F32, name="inv_gpsimd")
+            copy = nc.scalar.copy if l in SCALAR_SHARE else nc.vector.tensor_copy
+            copy(out=inv_gpsimd[l][:], in_=inv_rows[l][:, VECTOR_COLS:])
+
+        def scale_columns(engine, l, c, first, last, inv):
             engine.tensor_tensor(
-                out=nd[:, c, first:last, :].rearrange("p (n i) t -> p n t i", i=RUN),
+                out=nd[l][:, c, first:last, :].rearrange("p (n i) t -> p n t i", i=RUN),
                 in0=w_sb[l][:, c * PACK : (c + 1) * PACK, first:last].rearrange("p t (n i) -> p n t i", i=RUN),
                 in1=inv.rearrange("p (n i) -> p n i", i=RUN)
                 .unsqueeze(2)
@@ -110,83 +168,175 @@ def tile_npertokenswishglu_basis_pb_kernel(tc, h, w_down_mix, out):
                 op=ALU.mult,
             )
 
-        def quantise_weight(l, inv_rows):
-            nd = work.tile([P, PASSES, OUT, PACK], BF16, name="nd", align_bytes=64)
-            codes = work.tile([P, PASSES, OUT], U32, name="w_codes", align_bytes=64)
-            scales = work.tile([P, PASSES, OUT], U8, name="w_scales", align_bytes=64)
-            inv_gpsimd = work.tile([P, OUT - VECTOR_COLS], F32, name="inv_gpsimd")
-            nc.vector.tensor_copy(out=inv_gpsimd[:], in_=inv_rows[:, VECTOR_COLS:])
-            for c in range(PASSES):
-                scale_columns(nc.gpsimd, l, c, VECTOR_COLS, OUT, inv_gpsimd[:], nd)
-                scale_columns(nc.vector, l, c, 0, VECTOR_COLS, inv_rows[:, :VECTOR_COLS], nd)
-            for c in range(PASSES):
-                nc.vector.quantize_mx(
-                    out=codes[:, c, :].bitcast(FP8X4),
-                    scales=scales[:, c, :],
-                    in_=nd[:, c].rearrange("p j t -> p (j t)"),
-                )
-            return codes, scales
+        def scale_weight(l, c):
+            if c == 0:
+                nd[l] = work.tile([P, PASSES, OUT, PACK], BF16, name="nd", align_bytes=64)
+            scale_columns(nc.gpsimd, l, c, VECTOR_COLS, OUT, inv_gpsimd[l][:])
+            scale_columns(nc.vector, l, c, 0, VECTOR_COLS, inv_rows[l][:, :VECTOR_COLS])
+
+        def quantise_weight(l, c):
+            if c == 0:
+                w_codes[l] = work.tile([P, PASSES, OUT], U32, name="w_codes", align_bytes=64)
+                w_scales[l] = work.tile([P, PASSES, OUT], U8, name="w_scales", align_bytes=64)
+            nc.vector.quantize_mx(
+                out=w_codes[l][:, c, :].bitcast(FP8X4),
+                scales=w_scales[l][:, c, :],
+                in_=nd[l][:, c].rearrange("p j t -> p (j t)"),
+            )
+
+        def turn_hidden(l, c):
+            hT[l, c] = hT_psum.tile([P, HALVES, B_TILES, P], F32, name="hT")
+            for u in range(HALVES):
+                for i in range(B_TILES):
+                    words = h_sb[l][:, i, :].bitcast(F32)
+                    first = c * HALVES * P
+                    nc.tensor.transpose(
+                        hT[l, c][:, u, i, :], words[:, first + u : first + HALVES * P : HALVES], ident_f32[:]
+                    )
+
+        def group_hidden(l, c):
+            if c == 0:
+                grouped[l] = work.tile([P, PASSES * BATCH * PACK], BF16, name="h_grouped", align_bytes=64)
+            words = grouped[l][:].bitcast(F32).rearrange("p (c b u) -> p c b u", c=PASSES, u=HALVES)
+            copy = nc.scalar.copy if l >= SCALAR_HIDDEN else nc.vector.tensor_copy
+            copy(out=words[:, c], in_=hT[l, c][:].rearrange("p u i b -> p (i b) u"))
 
         def quantise_hidden(l):
-            h_tile = h_sb[l // TOKENS_PER_H_LOAD]
-            grouped = work.tile([P, PASSES * BATCH * PACK], BF16, name="h_grouped", align_bytes=64)
-            grouped_words = grouped[:].bitcast(F32).rearrange("p (c b u) -> p c b u", c=PASSES, u=HALVES)
+            h_codes[l] = work.tile([P, PASSES * BATCH], U32, name="h_codes", align_bytes=64)
+            h_scales[l] = work.tile([P, PASSES * BATCH], U8, name="h_scales", align_bytes=64)
+            nc.vector.quantize_mx(out=h_codes[l][:].bitcast(FP8X4), scales=h_scales[l][:], in_=grouped[l][:])
+
+        def project(l, i):
+            y[l, i] = y_psum.tile([P, OUT], F32, name="y")
             for c in range(PASSES):
-                hT = hT_psum.tile([P, HALVES, B_TILES, P], F32, name="hT")
-                for u in range(HALVES):
-                    for i in range(B_TILES):
-                        words = h_tile[:, i, l % TOKENS_PER_H_LOAD, :].bitcast(F32)
-                        first = c * HALVES * P
-                        nc.tensor.transpose(
-                            hT[:, u, i, :], words[:, first + u : first + HALVES * P : HALVES], ident_f32[:]
-                        )
-                nc.vector.tensor_copy(out=grouped_words[:, c], in_=hT[:].rearrange("p u i b -> p (i b) u"))
-            codes = h_mx.tile([P, PASSES * BATCH], U32, name="h_codes", align_bytes=64)
-            scales = h_mx.tile([P, PASSES * BATCH], U8, name="h_scales", align_bytes=64)
-            nc.vector.quantize_mx(out=codes[:].bitcast(FP8X4), scales=scales[:], in_=grouped[:])
-            return codes, scales
-
-        def project(l, h_q, w_q):
-            h_codes, h_scales = h_q
-            w_codes, w_scales = w_q
-            row_sq = small.tile([P, B_TILES], F32, name="row_sq")
-            y_tiles = []
-            for i in range(B_TILES):
-                y = y_psum.tile([P, OUT], F32, name="y")
-                for c in range(PASSES):
-                    b_cols = slice((c * B_TILES + i) * P, (c * B_TILES + i + 1) * P)
-                    nc.tensor.matmul_mx(
-                        out=y[:],
-                        lhsT=h_codes[:, b_cols].bitcast(FP8X4),
-                        lhsT_scale=h_scales[:, b_cols],
-                        rhs=w_codes[:, c, :].bitcast(FP8X4),
-                        rhs_scale=w_scales[:, c, :],
-                        start=(c == 0),
-                        stop=(c == PASSES - 1),
-                    )
-                y_squares = unread.tile([P, OUT], BF16, name="y_squares")
-                nc.scalar.activation(
-                    out=y_squares[:], in_=y[:], func=ACT.Square, accum_out=row_sq[:, i : i + 1]
+                b_cols = slice((c * B_TILES + i) * P, (c * B_TILES + i + 1) * P)
+                nc.tensor.matmul_mx(
+                    out=y[l, i][:],
+                    lhsT=h_codes[l][:, b_cols].bitcast(FP8X4),
+                    lhsT_scale=h_scales[l][:, b_cols],
+                    rhs=w_codes[l][:, c, :].bitcast(FP8X4),
+                    rhs_scale=w_scales[l][:, c, :],
+                    start=(c == 0),
+                    stop=(c == PASSES - 1),
                 )
-                y_tiles.append(y)
-            row_inv = inverse_norm(row_sq, B_TILES, "row")
-            unit = result.tile([P, B_TILES, OUT], F32, name="unit")
-            nc.scalar.activation(out=unit[:, 0, :], in_=y_tiles[0][:], func=ACT.Copy, scale=row_inv[:, 0:1])
-            nc.vector.tensor_scalar_mul(out=unit[:, 1, :], in0=y_tiles[1][:], scalar1=row_inv[:, 1:2])
-            nc.sync.dma_start(out=out.rearrange("(i p) l j -> p i l j", p=P)[:, :, l, :], in_=unit[:])
 
-        NORMS_AHEAD = 1
-        HIDDEN_AHEAD = 2
-        inv_rows = {}
-        h_q = {}
-        for l in range(NORMS_AHEAD):
-            inv_rows[l] = weight_norms(l)
-        for l in range(HIDDEN_AHEAD):
-            h_q[l] = quantise_hidden(l)
-        for l in range(TOKENS):
-            if l + NORMS_AHEAD < TOKENS:
-                inv_rows[l + NORMS_AHEAD] = weight_norms(l + NORMS_AHEAD)
-            if l + HIDDEN_AHEAD < TOKENS:
-                h_q[l + HIDDEN_AHEAD] = quantise_hidden(l + HIDDEN_AHEAD)
-            w_q = quantise_weight(l, inv_rows[l])
-            project(l, h_q[l], w_q)
+        def row_squares(l, i):
+            if i == 0:
+                row_sq[l] = small.tile([P, B_TILES], F32, name="row_sq")
+            y_squares = unread.tile([P, OUT], BF16, name="y_squares")
+            nc.scalar.activation(
+                out=y_squares[:], in_=y[l, i][:], func=ACT.Square, accum_out=row_sq[l][:, i : i + 1]
+            )
+
+        def unit_rows(l, i):
+            if i == 0:
+                unit[l] = result.tile([P, B_TILES, OUT], F32, name="unit")
+            if l >= SCALAR_UNIT[i]:
+                nc.scalar.activation(
+                    out=unit[l][:, i, :], in_=y[l, i][:], func=ACT.Copy, scale=row_inv[l][:, i : i + 1]
+                )
+            else:
+                nc.vector.tensor_scalar_mul(
+                    out=unit[l][:, i, :], in0=y[l, i][:], scalar1=row_inv[l][:, i : i + 1]
+                )
+
+        def store(l):
+            nc.sync.dma_start(out=out.rearrange("(i p) l j -> p i l j", p=P)[:, :, l, :], in_=unit[l][:])
+
+        for c in range(PASSES):
+            turn_weight(0, 0, [c])
+            for m in range(1, J_BLOCKS):
+                gram_products(0, m, c)
+        column_squares(0, 0)
+        for m in range(1, J_BLOCKS):
+            gram_diagonal(0, m)
+        turn_weight(1, 0)
+        col_inv[0] = invert(clamp(col_sq[0], "col"), "col")
+        gram_products(1, 1, 0)
+        gram_products(1, 1, 1)
+        spread_norms(0)
+        for m in range(2, J_BLOCKS):
+            for c in range(PASSES):
+                gram_products(1, m, c)
+        turn_hidden(0, 0)
+        share_norms(0)
+        scale_weight(0, 0)
+        column_squares(1, 0)
+        turn_weight(2, 0)
+        column_squares(2, 0)
+        scale_weight(0, 1)
+        turn_weight(2, 1)
+        column_squares(2, 1)
+        for m in range(1, J_BLOCKS):
+            gram_diagonal(1, m)
+        col_excess = {}
+        row_excess = {}
+        col_excess[1] = clamp(col_sq[1], "col")
+        turn_weight(2, 2)
+        group_hidden(0, 0)
+        turn_hidden(0, 1)
+        column_squares(2, 2)
+        col_inv[1] = invert(col_excess[1], "col")
+        quantise_weight(0, 0)
+        turn_weight(2, 3)
+        spread_norms(1)
+        group_hidden(0, 1)
+        share_norms(1)
+        column_squares(2, 3)
+        quantise_hidden(0)
+        for l in range(1, TOKENS + 1):
+            a = l + 2
+            if l < TOKENS:
+                scale_weight(l, 0)
+            if l > 1:
+                row_inv[l - 2] = invert(row_excess[l - 2], "row")
+            if l + 1 < TOKENS:
+                col_excess[l + 1] = clamp(col_sq[l + 1], "col")
+            if a < TOKENS:
+                turn_weight(a, 0)
+                column_squares(a, 0)
+            if l + 1 < TOKENS:
+                col_inv[l + 1] = invert(col_excess[l + 1], "col")
+            quantise_weight(l - 1, 1)
+            if a < TOKENS:
+                turn_weight(a, 1)
+            if l < TOKENS:
+                turn_hidden(l, 0)
+            project(l - 1, 0)
+            project(l - 1, 1)
+            if l > 1:
+                unit_rows(l - 2, 0)
+            if l < TOKENS:
+                scale_weight(l, 1)
+            if l > 1:
+                unit_rows(l - 2, 1)
+                store(l - 2)
+            if a < TOKENS:
+                column_squares(a, 1)
+                turn_weight(a, 2)
+            if l < TOKENS:
+                group_hidden(l, 0)
+            if a < TOKENS:
+                turn_weight(a, 3)
+            if l < TOKENS:
+                turn_hidden(l, 1)
+            row_squares(l - 1, 0)
+            row_squares(l - 1, 1)
+            if l + 1 < TOKENS:
+                spread_norms(l + 1)
+            if l < TOKENS:
+                quantise_weight(l, 0)
+                group_hidden(l, 1)
+            if a < TOKENS:
+                column_squares(a, 2)
+            row_excess[l - 1] = clamp(row_sq[l - 1], "row")
+            if l + 1 < TOKENS:
+                share_norms(l + 1)
+            if a < TOKENS:
+                column_squares(a, 3)
+            if l < TOKENS:
+                quantise_hidden(l)
+        row_inv[TOKENS - 1] = invert(row_excess[TOKENS - 1], "row")
+        unit_rows(TOKENS - 1, 0)
+        unit_rows(TOKENS - 1, 1)
+        store(TOKENS - 1)

@@ -21,12 +21,14 @@ B_TILES = BATCH // P
 J_BLOCKS = OUT // P
 EPS = 1e-12
 GRAM_TOKENS = 2
-VECTOR_COLS = 304
+VECTOR_COLS = [336,336,336,336,336,336,400,400]
+GPSIMD_CONTIG = True
+GPSIMD_WHOLE = False
 RUN = 4
 
-SCALAR_UNIT = (4, 4)
-SCALAR_HIDDEN = 6
-SCALAR_SHARE = (0,)
+SCALAR_UNIT = [(4,0),(4,1),(5,0),(5,1),(6,0),(6,1),(7,0)]
+SCALAR_HIDDEN = []
+SCALAR_SHARE = [0]
 FLOPS = 2 * BATCH * TOKENS * HIDDEN * OUT
 
 
@@ -40,10 +42,10 @@ def tile_npertokenswishglu_basis_pb_kernel(tc, h, w_down_mix, out):
         unread = stack.enter_context(tc.tile_pool(name="unread", bufs=2))
         small = stack.enter_context(tc.tile_pool(name="small", bufs=TOKENS))
         result = stack.enter_context(tc.tile_pool(name="result", bufs=3))
-        wT_psum = stack.enter_context(tc.psum_pool(name="wT_psum", bufs=2))
+        wT_psum = stack.enter_context(tc.psum_pool(name="wT_psum", bufs=3))
         inv_psum = stack.enter_context(tc.psum_pool(name="inv_psum", bufs=1))
         hT_psum = stack.enter_context(tc.psum_pool(name="hT_psum", bufs=2))
-        y_psum = stack.enter_context(tc.psum_pool(name="y_psum", bufs=3))
+        y_psum = stack.enter_context(tc.psum_pool(name="y_psum", bufs=2))
         stack.enter_context(tc.manual_schedule())
 
         ident_f32 = const.tile([P, P], F32, name="ident_f32")
@@ -106,6 +108,9 @@ def tile_npertokenswishglu_basis_pb_kernel(tc, h, w_down_mix, out):
             nc.scalar.activation(out=inv[:], in_=excess[:], func=ACT.Abs_reciprocal_sqrt, bias=EPS * EPS)
             return inv
 
+        def vector_cols(l):
+            return VECTOR_COLS[min(l, len(VECTOR_COLS) - 1)]
+
         def turn_weight(l, m, passes=range(PASSES)):
             if passes[0] == 0:
                 wT[l, m] = wT_psum.tile([P, ROWS, P], BF16, name="wT")
@@ -124,7 +129,9 @@ def tile_npertokenswishglu_basis_pb_kernel(tc, h, w_down_mix, out):
             )
 
         def gram_products(l, m, c):
-            if c == 0:
+            if c == 0 and (l, m) == (0, J_BLOCKS - 1):
+                gram[l, m] = hT_psum.tile([P, OUT], F32, name="hT")
+            elif c == 0:
                 gram[l, m] = y_psum.tile([P, OUT], F32, name="y")
             for r in range(c * PACK, (c + 1) * PACK):
                 block = w_sb[l][:, r, m * P : (m + 1) * P]
@@ -154,9 +161,10 @@ def tile_npertokenswishglu_basis_pb_kernel(tc, h, w_down_mix, out):
                 )
 
         def share_norms(l):
-            inv_gpsimd[l] = work.tile([P, OUT - VECTOR_COLS], F32, name="inv_gpsimd")
+            first = vector_cols(l)
+            inv_gpsimd[l] = work.tile([P, OUT - first], F32, name="inv_gpsimd")
             copy = nc.scalar.copy if l in SCALAR_SHARE else nc.vector.tensor_copy
-            copy(out=inv_gpsimd[l][:], in_=inv_rows[l][:, VECTOR_COLS:])
+            copy(out=inv_gpsimd[l][:], in_=inv_rows[l][:, first:])
 
         def scale_columns(engine, l, c, first, last, inv):
             engine.tensor_tensor(
@@ -171,8 +179,16 @@ def tile_npertokenswishglu_basis_pb_kernel(tc, h, w_down_mix, out):
         def scale_weight(l, c):
             if c == 0:
                 nd[l] = work.tile([P, PASSES, OUT, PACK], BF16, name="nd", align_bytes=64)
-            scale_columns(nc.gpsimd, l, c, VECTOR_COLS, OUT, inv_gpsimd[l][:])
-            scale_columns(nc.vector, l, c, 0, VECTOR_COLS, inv_rows[l][:, :VECTOR_COLS])
+            first = vector_cols(l)
+            if c == 0 or not GPSIMD_WHOLE:
+                passes = slice(0, PASSES) if GPSIMD_WHOLE else slice(c, c + 1)
+                nc.gpsimd.tensor_tensor(
+                    out=nd[l][:, passes, first:, :].rearrange("p c j t -> p j c t"),
+                    in0=w_sb[l][:, passes.start * PACK : passes.stop * PACK, first:].rearrange("p (c t) j -> p j c t", t=PACK),
+                    in1=inv_gpsimd[l][:].unsqueeze(2).unsqueeze(3).to_broadcast([P, OUT - first, passes.stop - passes.start, PACK]),
+                    op=ALU.mult,
+                ) if GPSIMD_CONTIG else scale_columns(nc.gpsimd, l, c, first, OUT, inv_gpsimd[l][:])
+            scale_columns(nc.vector, l, c, 0, first, inv_rows[l][:, :first])
 
         def quantise_weight(l, c):
             if c == 0:
@@ -198,7 +214,7 @@ def tile_npertokenswishglu_basis_pb_kernel(tc, h, w_down_mix, out):
             if c == 0:
                 grouped[l] = work.tile([P, PASSES * BATCH * PACK], BF16, name="h_grouped", align_bytes=64)
             words = grouped[l][:].bitcast(F32).rearrange("p (c b u) -> p c b u", c=PASSES, u=HALVES)
-            copy = nc.scalar.copy if l >= SCALAR_HIDDEN else nc.vector.tensor_copy
+            copy = nc.scalar.copy if l in SCALAR_HIDDEN else nc.vector.tensor_copy
             copy(out=words[:, c], in_=hT[l, c][:].rearrange("p u i b -> p (i b) u"))
 
         def quantise_hidden(l):
@@ -206,9 +222,10 @@ def tile_npertokenswishglu_basis_pb_kernel(tc, h, w_down_mix, out):
             h_scales[l] = work.tile([P, PASSES * BATCH], U8, name="h_scales", align_bytes=64)
             nc.vector.quantize_mx(out=h_codes[l][:].bitcast(FP8X4), scales=h_scales[l][:], in_=grouped[l][:])
 
-        def project(l, i):
-            y[l, i] = y_psum.tile([P, OUT], F32, name="y")
-            for c in range(PASSES):
+        def project(l, c):
+            for i in range(B_TILES):
+                if c == 0:
+                    y[l, i] = y_psum.tile([P, OUT], F32, name="y")
                 b_cols = slice((c * B_TILES + i) * P, (c * B_TILES + i + 1) * P)
                 nc.tensor.matmul_mx(
                     out=y[l, i][:],
@@ -231,7 +248,7 @@ def tile_npertokenswishglu_basis_pb_kernel(tc, h, w_down_mix, out):
         def unit_rows(l, i):
             if i == 0:
                 unit[l] = result.tile([P, B_TILES, OUT], F32, name="unit")
-            if l >= SCALAR_UNIT[i]:
+            if (l, i) in SCALAR_UNIT:
                 nc.scalar.activation(
                     out=unit[l][:, i, :], in_=y[l, i][:], func=ACT.Copy, scale=row_inv[l][:, i : i + 1]
                 )
@@ -243,6 +260,28 @@ def tile_npertokenswishglu_basis_pb_kernel(tc, h, w_down_mix, out):
         def store(l):
             nc.sync.dma_start(out=out.rearrange("(i p) l j -> p i l j", p=P)[:, :, l, :], in_=unit[l][:])
 
+        blocks = [(l, m) for l in range(1, TOKENS) for m in range(1 if l < GRAM_TOKENS else J_BLOCKS)]
+        to_turn = list(blocks)
+        to_square = list(blocks)
+        col_excess = {}
+        row_excess = {}
+
+        def turn_next():
+            if to_turn:
+                turn_weight(*to_turn.pop(0))
+
+        def square_next():
+            if to_square:
+                column_squares(*to_square.pop(0))
+
+        def clamp_columns(l):
+            if l < TOKENS:
+                col_excess[l] = clamp(col_sq[l], "col")
+
+        def invert_columns(l):
+            if l < TOKENS:
+                col_inv[l] = invert(col_excess[l], "col")
+
         for c in range(PASSES):
             turn_weight(0, 0, [c])
             for m in range(1, J_BLOCKS):
@@ -250,93 +289,82 @@ def tile_npertokenswishglu_basis_pb_kernel(tc, h, w_down_mix, out):
         column_squares(0, 0)
         for m in range(1, J_BLOCKS):
             gram_diagonal(0, m)
-        turn_weight(1, 0)
-        col_inv[0] = invert(clamp(col_sq[0], "col"), "col")
+        turn_next()
+        clamp_columns(0)
+        invert_columns(0)
         gram_products(1, 1, 0)
         gram_products(1, 1, 1)
         spread_norms(0)
-        for m in range(2, J_BLOCKS):
-            for c in range(PASSES):
-                gram_products(1, m, c)
+        gram_products(1, 2, 0)
+        gram_products(1, 2, 1)
         turn_hidden(0, 0)
-        share_norms(0)
-        scale_weight(0, 0)
-        column_squares(1, 0)
-        turn_weight(2, 0)
-        column_squares(2, 0)
-        scale_weight(0, 1)
-        turn_weight(2, 1)
-        column_squares(2, 1)
-        for m in range(1, J_BLOCKS):
-            gram_diagonal(1, m)
-        col_excess = {}
-        row_excess = {}
-        col_excess[1] = clamp(col_sq[1], "col")
-        turn_weight(2, 2)
-        group_hidden(0, 0)
         turn_hidden(0, 1)
-        column_squares(2, 2)
-        col_inv[1] = invert(col_excess[1], "col")
-        quantise_weight(0, 0)
-        turn_weight(2, 3)
-        spread_norms(1)
+        turn_next()
+        share_norms(0)
+        square_next()
+        scale_weight(0, 0)
+        square_next()
+        turn_next()
+        scale_weight(0, 1)
+        gram_diagonal(1, 1)
+        gram_diagonal(1, 2)
+        gram_products(1, 3, 0)
+        gram_products(1, 3, 1)
+        turn_next()
+        group_hidden(0, 0)
         group_hidden(0, 1)
-        share_norms(1)
-        column_squares(2, 3)
+        gram_diagonal(1, 3)
+        turn_hidden(1, 0)
+        turn_hidden(1, 1)
+        square_next()
+        clamp_columns(1)
+        turn_next()
+        square_next()
+        invert_columns(1)
+        spread_norms(1)
+        turn_next()
+        square_next()
+        group_hidden(1, 0)
+        group_hidden(1, 1)
+        turn_next()
+        for c in range(PASSES):
+            quantise_weight(0, c)
         quantise_hidden(0)
+        quantise_hidden(1)
         for l in range(1, TOKENS + 1):
-            a = l + 2
             if l < TOKENS:
+                share_norms(l)
                 scale_weight(l, 0)
-            if l > 1:
-                row_inv[l - 2] = invert(row_excess[l - 2], "row")
-            if l + 1 < TOKENS:
-                col_excess[l + 1] = clamp(col_sq[l + 1], "col")
-            if a < TOKENS:
-                turn_weight(a, 0)
-                column_squares(a, 0)
-            if l + 1 < TOKENS:
-                col_inv[l + 1] = invert(col_excess[l + 1], "col")
-            quantise_weight(l - 1, 1)
-            if a < TOKENS:
-                turn_weight(a, 1)
-            if l < TOKENS:
-                turn_hidden(l, 0)
-            project(l - 1, 0)
-            project(l - 1, 1)
-            if l > 1:
-                unit_rows(l - 2, 0)
-            if l < TOKENS:
-                scale_weight(l, 1)
-            if l > 1:
-                unit_rows(l - 2, 1)
-                store(l - 2)
-            if a < TOKENS:
-                column_squares(a, 1)
-                turn_weight(a, 2)
-            if l < TOKENS:
-                group_hidden(l, 0)
-            if a < TOKENS:
-                turn_weight(a, 3)
-            if l < TOKENS:
-                turn_hidden(l, 1)
+            for c in range(PASSES):
+                project(l - 1, c)
             row_squares(l - 1, 0)
             row_squares(l - 1, 1)
+            row_excess[l - 1] = clamp(row_sq[l - 1], "row")
+            clamp_columns(l + 1)
+            square_next()
+            turn_next()
+            row_inv[l - 1] = invert(row_excess[l - 1], "row")
+            invert_columns(l + 1)
+            if l < TOKENS:
+                scale_weight(l, 1)
+            if l + 1 < TOKENS:
+                turn_hidden(l + 1, 0)
+                turn_hidden(l + 1, 1)
+                group_hidden(l + 1, 0)
+                group_hidden(l + 1, 1)
+            square_next()
+            turn_next()
+            unit_rows(l - 1, 0)
+            unit_rows(l - 1, 1)
+            store(l - 1)
+            square_next()
             if l + 1 < TOKENS:
                 spread_norms(l + 1)
+            turn_next()
+            square_next()
+            turn_next()
             if l < TOKENS:
-                quantise_weight(l, 0)
-                group_hidden(l, 1)
-            if a < TOKENS:
-                column_squares(a, 2)
-            row_excess[l - 1] = clamp(row_sq[l - 1], "row")
+                for c in range(PASSES):
+                    quantise_weight(l, c)
             if l + 1 < TOKENS:
-                share_norms(l + 1)
-            if a < TOKENS:
-                column_squares(a, 3)
-            if l < TOKENS:
-                quantise_hidden(l)
-        row_inv[TOKENS - 1] = invert(row_excess[TOKENS - 1], "row")
-        unit_rows(TOKENS - 1, 0)
-        unit_rows(TOKENS - 1, 1)
-        store(TOKENS - 1)
+                quantise_hidden(l + 1)

@@ -21,9 +21,7 @@ B_TILES = BATCH // P
 J_BLOCKS = OUT // P
 EPS = 1e-12
 GRAM_TOKENS = 2
-VECTOR_COLS = [336,336,336,336,336,336,400,400]
-GPSIMD_CONTIG = True
-GPSIMD_WHOLE = False
+VECTOR_COLS = [304,304,304,304,304,336,384,448]
 RUN = 4
 
 SCALAR_UNIT = [(4,0),(4,1),(5,0),(5,1),(6,0),(6,1),(7,0)]
@@ -80,6 +78,9 @@ def tile_npertokenswishglu_basis_pb_kernel(tc, h, w_down_mix, out):
             if l >= WEIGHTS_FIRST - 1:
                 load_hidden(l - WEIGHTS_FIRST + 1)
 
+        warm = hT_psum.tile([P, OUT], F32, name="hT")
+        for n in range(3):
+            nc.tensor.matmul(out=warm[:, :P], lhsT=ident_f32[:], rhs=ident_f32[:], start=True, stop=True)
         wT = {}
         col_sq = {}
         col_inv = {}
@@ -107,9 +108,6 @@ def tile_npertokenswishglu_basis_pb_kernel(tc, h, w_down_mix, out):
             inv = small.tile([P, excess.shape[1]], F32, name=name + "_inv")
             nc.scalar.activation(out=inv[:], in_=excess[:], func=ACT.Abs_reciprocal_sqrt, bias=EPS * EPS)
             return inv
-
-        def vector_cols(l):
-            return VECTOR_COLS[min(l, len(VECTOR_COLS) - 1)]
 
         def turn_weight(l, m, passes=range(PASSES)):
             if passes[0] == 0:
@@ -151,6 +149,9 @@ def tile_npertokenswishglu_basis_pb_kernel(tc, h, w_down_mix, out):
                 accum_out=col_sq[l][:, m : m + 1],
             )
 
+        def vector_cols(l):
+            return VECTOR_COLS[min(l, len(VECTOR_COLS) - 1)]
+
         def spread_norms(l):
             inv_rows[l] = inv_psum.tile([P, OUT], F32, name="inv_rows")
             for m in range(J_BLOCKS):
@@ -180,14 +181,12 @@ def tile_npertokenswishglu_basis_pb_kernel(tc, h, w_down_mix, out):
             if c == 0:
                 nd[l] = work.tile([P, PASSES, OUT, PACK], BF16, name="nd", align_bytes=64)
             first = vector_cols(l)
-            if c == 0 or not GPSIMD_WHOLE:
-                passes = slice(0, PASSES) if GPSIMD_WHOLE else slice(c, c + 1)
-                nc.gpsimd.tensor_tensor(
-                    out=nd[l][:, passes, first:, :].rearrange("p c j t -> p j c t"),
-                    in0=w_sb[l][:, passes.start * PACK : passes.stop * PACK, first:].rearrange("p (c t) j -> p j c t", t=PACK),
-                    in1=inv_gpsimd[l][:].unsqueeze(2).unsqueeze(3).to_broadcast([P, OUT - first, passes.stop - passes.start, PACK]),
-                    op=ALU.mult,
-                ) if GPSIMD_CONTIG else scale_columns(nc.gpsimd, l, c, first, OUT, inv_gpsimd[l][:])
+            nc.gpsimd.tensor_tensor(
+                out=nd[l][:, c, first:, :],
+                in0=w_sb[l][:, c * PACK : (c + 1) * PACK, first:].rearrange("p t j -> p j t"),
+                in1=inv_gpsimd[l][:].unsqueeze(2).to_broadcast([P, OUT - first, PACK]),
+                op=ALU.mult,
+            )
             scale_columns(nc.vector, l, c, 0, first, inv_rows[l][:, :first])
 
         def quantise_weight(l, c):
@@ -257,10 +256,13 @@ def tile_npertokenswishglu_basis_pb_kernel(tc, h, w_down_mix, out):
                     out=unit[l][:, i, :], in0=y[l, i][:], scalar1=row_inv[l][:, i : i + 1]
                 )
 
+        def store_half(l, i):
+            nc.sync.dma_start(out=out.rearrange("(i p) l j -> p i l j", p=P)[:, i, l, :], in_=unit[l][:, i, :])
+
         def store(l):
             nc.sync.dma_start(out=out.rearrange("(i p) l j -> p i l j", p=P)[:, :, l, :], in_=unit[l][:])
 
-        blocks = [(l, m) for l in range(1, TOKENS) for m in range(1 if l < GRAM_TOKENS else J_BLOCKS)]
+        blocks = [(l, m) for l in range(1, TOKENS) for m in range(min(l + 1, J_BLOCKS))]
         to_turn = list(blocks)
         to_square = list(blocks)
         col_excess = {}
@@ -292,64 +294,64 @@ def tile_npertokenswishglu_basis_pb_kernel(tc, h, w_down_mix, out):
         turn_next()
         clamp_columns(0)
         invert_columns(0)
-        gram_products(1, 1, 0)
-        gram_products(1, 1, 1)
-        spread_norms(0)
-        gram_products(1, 2, 0)
-        gram_products(1, 2, 1)
-        turn_hidden(0, 0)
-        turn_hidden(0, 1)
         turn_next()
+        spread_norms(0)
         share_norms(0)
         square_next()
-        scale_weight(0, 0)
+        for m in range(2, J_BLOCKS):
+            gram_products(1, m, 0)
+            gram_products(1, m, 1)
+        turn_hidden(0, 0)
+        turn_hidden(0, 1)
         square_next()
+        scale_weight(0, 0)
         turn_next()
         scale_weight(0, 1)
-        gram_diagonal(1, 1)
+        square_next()
         gram_diagonal(1, 2)
-        gram_products(1, 3, 0)
-        gram_products(1, 3, 1)
-        turn_next()
+        gram_diagonal(1, 3)
         group_hidden(0, 0)
         group_hidden(0, 1)
-        gram_diagonal(1, 3)
+        turn_next()
+        gram_products(2, 3, 0)
+        gram_products(2, 3, 1)
         turn_hidden(1, 0)
         turn_hidden(1, 1)
-        square_next()
         clamp_columns(1)
-        turn_next()
         square_next()
         invert_columns(1)
-        spread_norms(1)
         turn_next()
-        square_next()
+        spread_norms(1)
         group_hidden(1, 0)
         group_hidden(1, 1)
+        gram_diagonal(2, 3)
+        square_next()
         turn_next()
         for c in range(PASSES):
             quantise_weight(0, c)
         quantise_hidden(0)
         quantise_hidden(1)
-        for l in range(1, TOKENS + 1):
-            if l < TOKENS:
-                share_norms(l)
-                scale_weight(l, 0)
+        for l in range(1, TOKENS):
+            share_norms(l)
+            scale_weight(l, 0)
             for c in range(PASSES):
                 project(l - 1, c)
+            if l + 1 < TOKENS:
+                turn_hidden(l + 1, 0)
+                turn_hidden(l + 1, 1)
+            turn_next()
             row_squares(l - 1, 0)
             row_squares(l - 1, 1)
             row_excess[l - 1] = clamp(row_sq[l - 1], "row")
             clamp_columns(l + 1)
-            square_next()
-            turn_next()
             row_inv[l - 1] = invert(row_excess[l - 1], "row")
             invert_columns(l + 1)
-            if l < TOKENS:
-                scale_weight(l, 1)
+            square_next()
+            turn_next()
+            if l + 1 == TOKENS:
+                quantise_weight(l, 0)
+            scale_weight(l, 1)
             if l + 1 < TOKENS:
-                turn_hidden(l + 1, 0)
-                turn_hidden(l + 1, 1)
                 group_hidden(l + 1, 0)
                 group_hidden(l + 1, 1)
             square_next()
@@ -362,9 +364,17 @@ def tile_npertokenswishglu_basis_pb_kernel(tc, h, w_down_mix, out):
                 spread_norms(l + 1)
             turn_next()
             square_next()
-            turn_next()
-            if l < TOKENS:
+            if l + 1 < TOKENS:
                 for c in range(PASSES):
                     quantise_weight(l, c)
-            if l + 1 < TOKENS:
                 quantise_hidden(l + 1)
+        last = TOKENS - 1
+        project(last, 0)
+        quantise_weight(last, 1)
+        project(last, 1)
+        for i in range(B_TILES):
+            row_squares(last, i)
+        row_inv[last] = invert(clamp(row_sq[last], "row"), "row")
+        for i in range(B_TILES):
+            unit_rows(last, i)
+            store_half(last, i)

@@ -20,12 +20,12 @@ HALVES = 2
 B_TILES = BATCH // P
 J_BLOCKS = OUT // P
 EPS = 1e-12
-GRAM_TOKENS = 2
+GRAM_FROM = [0, 2]
 VECTOR_COLS = [304,304,304,304,304,336,384,448]
 RUN = 4
 
 SCALAR_UNIT = [(4,0),(4,1),(5,0),(5,1),(6,0),(6,1),(7,0)]
-SCALAR_HIDDEN = []
+SCALAR_HIDDEN = [7]
 SCALAR_SHARE = [0]
 FLOPS = 2 * BATCH * TOKENS * HIDDEN * OUT
 
@@ -127,7 +127,7 @@ def tile_npertokenswishglu_basis_pb_kernel(tc, h, w_down_mix, out):
             )
 
         def gram_products(l, m, c):
-            if c == 0 and (l, m) == (0, J_BLOCKS - 1):
+            if c == 0 and l == 0 and m >= 2:
                 gram[l, m] = hT_psum.tile([P, OUT], F32, name="hT")
             elif c == 0:
                 gram[l, m] = y_psum.tile([P, OUT], F32, name="y")
@@ -154,6 +154,16 @@ def tile_npertokenswishglu_basis_pb_kernel(tc, h, w_down_mix, out):
 
         def spread_norms(l):
             inv_rows[l] = inv_psum.tile([P, OUT], F32, name="inv_rows")
+            for n in range(2 if l >= 2 else 0):
+                nc.tensor.matmul_mx(
+                    out=inv_rows[l][:],
+                    lhsT=h_codes[l - 2][:, :P].bitcast(FP8X4),
+                    lhsT_scale=h_scales[l - 2][:, :P],
+                    rhs=w_codes[l - 2][:, 0, :].bitcast(FP8X4),
+                    rhs_scale=w_scales[l - 2][:, 0, :],
+                    start=True,
+                    stop=True,
+                )
             for m in range(J_BLOCKS):
                 nc.tensor.transpose(
                     inv_rows[l][:, m * P : (m + 1) * P],
@@ -262,7 +272,8 @@ def tile_npertokenswishglu_basis_pb_kernel(tc, h, w_down_mix, out):
         def store(l):
             nc.sync.dma_start(out=out.rearrange("(i p) l j -> p i l j", p=P)[:, :, l, :], in_=unit[l][:])
 
-        blocks = [(l, m) for l in range(1, TOKENS) for m in range(min(l + 1, J_BLOCKS))]
+        blocks = [(l, m) for l in range(1, TOKENS) for m in range(2 if l < len(GRAM_FROM) else J_BLOCKS)]
+        col_sq[0] = small.tile([P, J_BLOCKS], F32, name="col_sq")
         to_turn = list(blocks)
         to_square = list(blocks)
         col_excess = {}
@@ -285,51 +296,47 @@ def tile_npertokenswishglu_basis_pb_kernel(tc, h, w_down_mix, out):
                 col_inv[l] = invert(col_excess[l], "col")
 
         for c in range(PASSES):
-            turn_weight(0, 0, [c])
-            for m in range(1, J_BLOCKS):
+            for m in range(J_BLOCKS):
                 gram_products(0, m, c)
-        column_squares(0, 0)
-        for m in range(1, J_BLOCKS):
+        for m in range(J_BLOCKS):
             gram_diagonal(0, m)
-        turn_next()
         clamp_columns(0)
         invert_columns(0)
-        turn_next()
         spread_norms(0)
         share_norms(0)
+        turn_next()
+        turn_next()
+        square_next()
         square_next()
         for m in range(2, J_BLOCKS):
             gram_products(1, m, 0)
             gram_products(1, m, 1)
         turn_hidden(0, 0)
         turn_hidden(0, 1)
-        square_next()
         scale_weight(0, 0)
-        turn_next()
         scale_weight(0, 1)
-        square_next()
+        turn_next()
         gram_diagonal(1, 2)
         gram_diagonal(1, 3)
+        clamp_columns(1)
+        invert_columns(1)
+        square_next()
+        turn_next()
         group_hidden(0, 0)
         group_hidden(0, 1)
         turn_next()
-        gram_products(2, 3, 0)
-        gram_products(2, 3, 1)
         turn_hidden(1, 0)
         turn_hidden(1, 1)
-        clamp_columns(1)
-        square_next()
-        invert_columns(1)
-        turn_next()
         spread_norms(1)
+        square_next()
         group_hidden(1, 0)
         group_hidden(1, 1)
-        gram_diagonal(2, 3)
-        square_next()
-        turn_next()
+        for n in range(3):
+            square_next()
+            turn_next()
+        quantise_hidden(0)
         for c in range(PASSES):
             quantise_weight(0, c)
-        quantise_hidden(0)
         quantise_hidden(1)
         for l in range(1, TOKENS):
             share_norms(l)
@@ -347,21 +354,20 @@ def tile_npertokenswishglu_basis_pb_kernel(tc, h, w_down_mix, out):
             row_inv[l - 1] = invert(row_excess[l - 1], "row")
             invert_columns(l + 1)
             square_next()
-            turn_next()
             if l + 1 == TOKENS:
                 quantise_weight(l, 0)
             scale_weight(l, 1)
             if l + 1 < TOKENS:
+                spread_norms(l + 1)
                 group_hidden(l + 1, 0)
                 group_hidden(l + 1, 1)
+            turn_next()
             square_next()
             turn_next()
             unit_rows(l - 1, 0)
             unit_rows(l - 1, 1)
             store(l - 1)
             square_next()
-            if l + 1 < TOKENS:
-                spread_norms(l + 1)
             turn_next()
             square_next()
             if l + 1 < TOKENS:

@@ -21,10 +21,10 @@ B_TILES = BATCH // P
 J_BLOCKS = OUT // P
 EPS = 1e-12
 GRAM_FROM = [0, 2]
-VECTOR_COLS = [304,304,304,304,304,336,384,448]
+VECTOR_COLS = [304,304,304,304,304,336,384,384]
 RUN = 4
 
-SCALAR_UNIT = [(4,0),(4,1),(5,0),(5,1),(6,0),(6,1),(7,0)]
+SCALAR_UNIT = [(4,0),(5,0),(5,1),(6,0),(6,1),(7,0)]
 SCALAR_HIDDEN = [7]
 SCALAR_SHARE = [0]
 FLOPS = 2 * BATCH * TOKENS * HIDDEN * OUT
@@ -71,12 +71,13 @@ def tile_npertokenswishglu_basis_pb_kernel(tc, h, w_down_mix, out):
             h_sb[l] = h_pool.tile([P, B_TILES, HIDDEN], BF16, name="h_tile")
             nc.sync.dma_start(out=h_sb[l][:], in_=h_view[:, :, l, :])
 
-        WEIGHTS_FIRST = 2
-        for l in range(TOKENS + WEIGHTS_FIRST - 1):
-            if l < TOKENS:
-                load_weight(l, PASSES if l == 0 else 1)
-            if l >= WEIGHTS_FIRST - 1:
-                load_hidden(l - WEIGHTS_FIRST + 1)
+        load_weight(0, PASSES)
+        load_weight(1, 1)
+        load_hidden(0)
+        load_hidden(1)
+        for l in range(2, TOKENS):
+            load_weight(l, 1)
+            load_hidden(l)
 
         warm = hT_psum.tile([P, OUT], F32, name="hT")
         for n in range(3):
@@ -116,8 +117,6 @@ def tile_npertokenswishglu_basis_pb_kernel(tc, h, w_down_mix, out):
                 nc.tensor.transpose(wT[l, m][:, r, :], w_sb[l][:, r, m * P : (m + 1) * P], ident_bf[:])
 
         def column_squares(l, m):
-            if l not in col_sq:
-                col_sq[l] = small.tile([P, J_BLOCKS], F32, name="col_sq")
             squares = unread.tile([P, ROWS * P], BF16, name="squares")
             nc.scalar.activation(
                 out=squares[:],
@@ -157,10 +156,10 @@ def tile_npertokenswishglu_basis_pb_kernel(tc, h, w_down_mix, out):
             for n in range(2 if l >= 2 else 0):
                 nc.tensor.matmul_mx(
                     out=inv_rows[l][:],
-                    lhsT=h_codes[l - 2][:, :P].bitcast(FP8X4),
-                    lhsT_scale=h_scales[l - 2][:, :P],
-                    rhs=w_codes[l - 2][:, 0, :].bitcast(FP8X4),
-                    rhs_scale=w_scales[l - 2][:, 0, :],
+                    lhsT=h_codes[l - 1][:, :P].bitcast(FP8X4),
+                    lhsT_scale=h_scales[l - 1][:, :P],
+                    rhs=h_codes[l - 1][:].bitcast(FP8X4),
+                    rhs_scale=h_scales[l - 1][:],
                     start=True,
                     stop=True,
                 )
@@ -233,7 +232,9 @@ def tile_npertokenswishglu_basis_pb_kernel(tc, h, w_down_mix, out):
 
         def project(l, c):
             for i in range(B_TILES):
-                if c == 0:
+                if c == 0 and l >= 6:
+                    y[l, i] = wT_psum.tile([P, OUT], F32, name="wT")
+                elif c == 0:
                     y[l, i] = y_psum.tile([P, OUT], F32, name="y")
                 b_cols = slice((c * B_TILES + i) * P, (c * B_TILES + i + 1) * P)
                 nc.tensor.matmul_mx(
@@ -246,9 +247,20 @@ def tile_npertokenswishglu_basis_pb_kernel(tc, h, w_down_mix, out):
                     stop=(c == PASSES - 1),
                 )
 
+        def keep_warm(l, passes):
+            for n in range(passes):
+                idle = hT_psum.tile([P, OUT], F32, name="hT")
+                nc.tensor.matmul_mx(
+                    out=idle[:],
+                    lhsT=h_codes[l][:, :P].bitcast(FP8X4),
+                    lhsT_scale=h_scales[l][:, :P],
+                    rhs=h_codes[l][:].bitcast(FP8X4),
+                    rhs_scale=h_scales[l][:],
+                    start=True,
+                    stop=True,
+                )
+
         def row_squares(l, i):
-            if i == 0:
-                row_sq[l] = small.tile([P, B_TILES], F32, name="row_sq")
             y_squares = unread.tile([P, OUT], BF16, name="y_squares")
             nc.scalar.activation(
                 out=y_squares[:], in_=y[l, i][:], func=ACT.Square, accum_out=row_sq[l][:, i : i + 1]
@@ -273,7 +285,20 @@ def tile_npertokenswishglu_basis_pb_kernel(tc, h, w_down_mix, out):
             nc.sync.dma_start(out=out.rearrange("(i p) l j -> p i l j", p=P)[:, :, l, :], in_=unit[l][:])
 
         blocks = [(l, m) for l in range(1, TOKENS) for m in range(2 if l < len(GRAM_FROM) else J_BLOCKS)]
-        col_sq[0] = small.tile([P, J_BLOCKS], F32, name="col_sq")
+        sums = {}
+        for l in range(-1, TOKENS + 1):
+            columns = J_BLOCKS if l + 1 < TOKENS else 0
+            rows = B_TILES if l > 0 else 0
+            sums[l] = small.tile([P, columns + rows], F32, name="sums%d" % l)
+            col_sq[l + 1] = sums[l][:, :columns]
+            row_sq[l - 1] = sums[l][:, columns:]
+
+        def invert_sums(l):
+            inv = invert(clamp(sums[l], "sums"), "sums")
+            columns = J_BLOCKS if l + 1 < TOKENS else 0
+            col_inv[l + 1] = inv[:, :columns]
+            row_inv[l - 1] = inv[:, columns:]
+
         to_turn = list(blocks)
         to_square = list(blocks)
         col_excess = {}
@@ -300,8 +325,7 @@ def tile_npertokenswishglu_basis_pb_kernel(tc, h, w_down_mix, out):
                 gram_products(0, m, c)
         for m in range(J_BLOCKS):
             gram_diagonal(0, m)
-        clamp_columns(0)
-        invert_columns(0)
+        invert_sums(-1)
         spread_norms(0)
         share_norms(0)
         turn_next()
@@ -315,23 +339,22 @@ def tile_npertokenswishglu_basis_pb_kernel(tc, h, w_down_mix, out):
         turn_hidden(0, 1)
         scale_weight(0, 0)
         scale_weight(0, 1)
-        turn_next()
         gram_diagonal(1, 2)
         gram_diagonal(1, 3)
-        clamp_columns(1)
-        invert_columns(1)
-        square_next()
-        turn_next()
+        invert_sums(0)
         group_hidden(0, 0)
         group_hidden(0, 1)
         turn_next()
+        square_next()
         turn_hidden(1, 0)
         turn_hidden(1, 1)
+        turn_next()
         spread_norms(1)
         square_next()
         group_hidden(1, 0)
         group_hidden(1, 1)
-        for n in range(3):
+        turn_next()
+        for n in range(2):
             square_next()
             turn_next()
         quantise_hidden(0)
@@ -347,18 +370,17 @@ def tile_npertokenswishglu_basis_pb_kernel(tc, h, w_down_mix, out):
                 turn_hidden(l + 1, 0)
                 turn_hidden(l + 1, 1)
             turn_next()
+            if l + 1 in SCALAR_HIDDEN:
+                group_hidden(l + 1, 0)
+                group_hidden(l + 1, 1)
             row_squares(l - 1, 0)
             row_squares(l - 1, 1)
-            row_excess[l - 1] = clamp(row_sq[l - 1], "row")
-            clamp_columns(l + 1)
-            row_inv[l - 1] = invert(row_excess[l - 1], "row")
-            invert_columns(l + 1)
+            invert_sums(l)
             square_next()
-            if l + 1 == TOKENS:
-                quantise_weight(l, 0)
             scale_weight(l, 1)
             if l + 1 < TOKENS:
                 spread_norms(l + 1)
+            if l + 1 < TOKENS and l + 1 not in SCALAR_HIDDEN:
                 group_hidden(l + 1, 0)
                 group_hidden(l + 1, 1)
             turn_next()
@@ -368,6 +390,8 @@ def tile_npertokenswishglu_basis_pb_kernel(tc, h, w_down_mix, out):
             unit_rows(l - 1, 1)
             store(l - 1)
             square_next()
+            if l + 2 < TOKENS:
+                keep_warm(l, 2)
             turn_next()
             square_next()
             if l + 1 < TOKENS:
@@ -375,12 +399,12 @@ def tile_npertokenswishglu_basis_pb_kernel(tc, h, w_down_mix, out):
                     quantise_weight(l, c)
                 quantise_hidden(l + 1)
         last = TOKENS - 1
-        project(last, 0)
-        quantise_weight(last, 1)
-        project(last, 1)
+        for c in range(PASSES):
+            quantise_weight(last, c)
+            project(last, c)
         for i in range(B_TILES):
             row_squares(last, i)
-        row_inv[last] = invert(clamp(row_sq[last], "row"), "row")
+        invert_sums(TOKENS)
         for i in range(B_TILES):
             unit_rows(last, i)
             store_half(last, i)

@@ -21,12 +21,14 @@ B_TILES = BATCH // P
 J_BLOCKS = OUT // P
 EPS = 1e-12
 GRAM_FROM = [0, 2]
-VECTOR_COLS = [304,304,304,304,304,336,384,384]
+VECTOR_COLS = [304]*6+[320,352]
 RUN = 4
 
-SCALAR_UNIT = [(4,0),(5,0),(5,1),(6,0),(6,1),(7,0)]
-SCALAR_HIDDEN = [7]
-SCALAR_SHARE = [0]
+SCALAR_UNIT = [(l, 0) for l in range(8)] + [(5, 1), (6, 1)]
+SCALAR_HIDDEN = []
+SCALAR_SHARE = [0, 7]
+W1, W2, W3 = 0, 0, 8
+SW = 2
 FLOPS = 2 * BATCH * TOKENS * HIDDEN * OUT
 
 
@@ -71,12 +73,8 @@ def tile_npertokenswishglu_basis_pb_kernel(tc, h, w_down_mix, out):
             h_sb[l] = h_pool.tile([P, B_TILES, HIDDEN], BF16, name="h_tile")
             nc.sync.dma_start(out=h_sb[l][:], in_=h_view[:, :, l, :])
 
-        load_weight(0, PASSES)
-        load_weight(1, 1)
-        load_hidden(0)
-        load_hidden(1)
-        for l in range(2, TOKENS):
-            load_weight(l, 1)
+        for l in range(TOKENS):
+            load_weight(l, PASSES if l == 0 else 1)
             load_hidden(l)
 
         warm = hT_psum.tile([P, OUT], F32, name="hT")
@@ -127,7 +125,7 @@ def tile_npertokenswishglu_basis_pb_kernel(tc, h, w_down_mix, out):
 
         def gram_products(l, m, c):
             if c == 0 and l == 0 and m >= 2:
-                gram[l, m] = hT_psum.tile([P, OUT], F32, name="hT")
+                gram[l, m] = wT_psum.tile([P, OUT], F32, name="wT")
             elif c == 0:
                 gram[l, m] = y_psum.tile([P, OUT], F32, name="y")
             for r in range(c * PACK, (c + 1) * PACK):
@@ -151,11 +149,11 @@ def tile_npertokenswishglu_basis_pb_kernel(tc, h, w_down_mix, out):
         def vector_cols(l):
             return VECTOR_COLS[min(l, len(VECTOR_COLS) - 1)]
 
-        def spread_norms(l):
-            inv_rows[l] = inv_psum.tile([P, OUT], F32, name="inv_rows")
-            for n in range(2 if l >= 2 else 0):
+        def spread_norms(l, blocks=range(J_BLOCKS)):
+            bank = wT_psum.tile([P, OUT], F32, name="wT") if blocks[0] or l == TOKENS - 1 else inv_psum.tile([P, OUT], F32, name="inv_rows")
+            for n in range(SW if l >= 2 else 0):
                 nc.tensor.matmul_mx(
-                    out=inv_rows[l][:],
+                    out=bank[:],
                     lhsT=h_codes[l - 1][:, :P].bitcast(FP8X4),
                     lhsT_scale=h_scales[l - 1][:, :P],
                     rhs=h_codes[l - 1][:].bitcast(FP8X4),
@@ -163,9 +161,10 @@ def tile_npertokenswishglu_basis_pb_kernel(tc, h, w_down_mix, out):
                     start=True,
                     stop=True,
                 )
-            for m in range(J_BLOCKS):
+            for m in blocks:
+                inv_rows[l, m] = bank
                 nc.tensor.transpose(
-                    inv_rows[l][:, m * P : (m + 1) * P],
+                    bank[:, m * P : (m + 1) * P],
                     col_inv[l][:, m : m + 1].to_broadcast([P, P]),
                     ident_f32[:],
                 )
@@ -174,7 +173,7 @@ def tile_npertokenswishglu_basis_pb_kernel(tc, h, w_down_mix, out):
             first = vector_cols(l)
             inv_gpsimd[l] = work.tile([P, OUT - first], F32, name="inv_gpsimd")
             copy = nc.scalar.copy if l in SCALAR_SHARE else nc.vector.tensor_copy
-            copy(out=inv_gpsimd[l][:], in_=inv_rows[l][:, first:])
+            copy(out=inv_gpsimd[l][:], in_=inv_rows[l, J_BLOCKS - 1][:, first:])
 
         def scale_columns(engine, l, c, first, last, inv):
             engine.tensor_tensor(
@@ -196,7 +195,8 @@ def tile_npertokenswishglu_basis_pb_kernel(tc, h, w_down_mix, out):
                 in1=inv_gpsimd[l][:].unsqueeze(2).to_broadcast([P, OUT - first, PACK]),
                 op=ALU.mult,
             )
-            scale_columns(nc.vector, l, c, 0, first, inv_rows[l][:, :first])
+            if l > 0:
+                scale_columns(nc.vector, l, c, 0, first, inv_rows[l, 0][:, :first])
 
         def quantise_weight(l, c):
             if c == 0:
@@ -247,11 +247,10 @@ def tile_npertokenswishglu_basis_pb_kernel(tc, h, w_down_mix, out):
                     stop=(c == PASSES - 1),
                 )
 
-        def keep_warm(l, passes):
+        def keep_warm(l, bank, passes):
             for n in range(passes):
-                idle = hT_psum.tile([P, OUT], F32, name="hT")
                 nc.tensor.matmul_mx(
-                    out=idle[:],
+                    out=bank[:],
                     lhsT=h_codes[l][:, :P].bitcast(FP8X4),
                     lhsT_scale=h_scales[l][:, :P],
                     rhs=h_codes[l][:].bitcast(FP8X4),
@@ -286,17 +285,22 @@ def tile_npertokenswishglu_basis_pb_kernel(tc, h, w_down_mix, out):
 
         blocks = [(l, m) for l in range(1, TOKENS) for m in range(2 if l < len(GRAM_FROM) else J_BLOCKS)]
         sums = {}
+        last = TOKENS - 1
         for l in range(-1, TOKENS + 1):
-            columns = J_BLOCKS if l + 1 < TOKENS else 0
+            columns = J_BLOCKS if l + 1 < last else 0
             rows = B_TILES if l > 0 else 0
             sums[l] = small.tile([P, columns + rows], F32, name="sums%d" % l)
-            col_sq[l + 1] = sums[l][:, :columns]
-            row_sq[l - 1] = sums[l][:, columns:]
+            if columns:
+                col_sq[l + 1] = sums[l][:, :columns]
+            if rows:
+                row_sq[l - 1] = sums[l][:, columns:]
+        col_sq[last] = small.tile([P, J_BLOCKS], F32, name="last_col_sq")
 
         def invert_sums(l):
             inv = invert(clamp(sums[l], "sums"), "sums")
-            columns = J_BLOCKS if l + 1 < TOKENS else 0
-            col_inv[l + 1] = inv[:, :columns]
+            columns = J_BLOCKS if l + 1 < last else 0
+            if columns:
+                col_inv[l + 1] = inv[:, :columns]
             row_inv[l - 1] = inv[:, columns:]
 
         to_turn = list(blocks)
@@ -325,9 +329,30 @@ def tile_npertokenswishglu_basis_pb_kernel(tc, h, w_down_mix, out):
                 gram_products(0, m, c)
         for m in range(J_BLOCKS):
             gram_diagonal(0, m)
-        invert_sums(-1)
-        spread_norms(0)
+        HALF = J_BLOCKS // 2
+        col_inv[0] = small.tile([P, J_BLOCKS], F32, name="col_inv0")
+        def inv_half(k):
+            cols = slice(k * HALF, (k + 1) * HALF)
+            ex = small.tile([P, HALF], F32, name="exh")
+            nc.scalar.activation(out=ex[:], in_=sums[-1][:, cols], func=ACT.Relu, bias=-EPS * EPS)
+            nc.scalar.activation(out=col_inv[0][:, cols], in_=ex[:], func=ACT.Abs_reciprocal_sqrt, bias=EPS * EPS)
+        inv_half(0)
+        turn_hidden(0, 0)
+        spread_norms(0, range(HALF))
+        inv_half(1)
+        spread_norms(0, range(HALF, J_BLOCKS))
         share_norms(0)
+        group_hidden(0, 0)
+        turn_hidden(0, 1)
+        scale_weight(0, 0)
+        scale_weight(0, 1)
+        mid = HALF * P
+        for c in range(PASSES):
+            scale_columns(nc.vector, 0, c, 0, mid, inv_rows[0, 0][:, :mid])
+        if vector_cols(0) > mid:
+            for c in range(PASSES):
+                scale_columns(nc.vector, 0, c, mid, vector_cols(0), inv_rows[0, HALF][:, mid:vector_cols(0)])
+        group_hidden(0, 1)
         turn_next()
         turn_next()
         square_next()
@@ -335,54 +360,43 @@ def tile_npertokenswishglu_basis_pb_kernel(tc, h, w_down_mix, out):
         for m in range(2, J_BLOCKS):
             gram_products(1, m, 0)
             gram_products(1, m, 1)
-        turn_hidden(0, 0)
-        turn_hidden(0, 1)
-        scale_weight(0, 0)
-        scale_weight(0, 1)
+        turn_hidden(1, 0)
+        turn_hidden(1, 1)
         gram_diagonal(1, 2)
         gram_diagonal(1, 3)
         invert_sums(0)
-        group_hidden(0, 0)
-        group_hidden(0, 1)
-        turn_next()
-        square_next()
-        turn_hidden(1, 0)
-        turn_hidden(1, 1)
+        group_hidden(1, 0)
         turn_next()
         spread_norms(1)
-        square_next()
-        group_hidden(1, 0)
         group_hidden(1, 1)
-        turn_next()
-        for n in range(2):
-            square_next()
-            turn_next()
         quantise_hidden(0)
+        square_next()
+        turn_next()
+        square_next()
+        turn_next()
+        square_next()
+        turn_next()
+        square_next()
+        turn_next()
         for c in range(PASSES):
             quantise_weight(0, c)
         quantise_hidden(1)
-        for l in range(1, TOKENS):
+        for l in range(1, last - 1):
             share_norms(l)
             scale_weight(l, 0)
             for c in range(PASSES):
                 project(l - 1, c)
-            if l + 1 < TOKENS:
-                turn_hidden(l + 1, 0)
-                turn_hidden(l + 1, 1)
+            turn_hidden(l + 1, 0)
+            turn_hidden(l + 1, 1)
             turn_next()
-            if l + 1 in SCALAR_HIDDEN:
-                group_hidden(l + 1, 0)
-                group_hidden(l + 1, 1)
             row_squares(l - 1, 0)
             row_squares(l - 1, 1)
             invert_sums(l)
             square_next()
             scale_weight(l, 1)
-            if l + 1 < TOKENS:
-                spread_norms(l + 1)
-            if l + 1 < TOKENS and l + 1 not in SCALAR_HIDDEN:
-                group_hidden(l + 1, 0)
-                group_hidden(l + 1, 1)
+            spread_norms(l + 1)
+            group_hidden(l + 1, 0)
+            group_hidden(l + 1, 1)
             turn_next()
             square_next()
             turn_next()
@@ -390,20 +404,55 @@ def tile_npertokenswishglu_basis_pb_kernel(tc, h, w_down_mix, out):
             unit_rows(l - 1, 1)
             store(l - 1)
             square_next()
-            if l + 2 < TOKENS:
-                keep_warm(l, 2)
             turn_next()
             square_next()
-            if l + 1 < TOKENS:
-                for c in range(PASSES):
-                    quantise_weight(l, c)
-                quantise_hidden(l + 1)
-        last = TOKENS - 1
+            for c in range(PASSES):
+                quantise_weight(l, c)
+            quantise_hidden(l + 1)
+        while to_turn:
+            turn_next()
+        while to_square:
+            square_next()
+        col_inv[last] = invert(clamp(col_sq[last], "col"), "col")
+        a = last - 1
+        share_norms(a)
+        scale_weight(a, 0)
+        for c in range(PASSES):
+            project(a - 1, c)
+        turn_hidden(last, 0)
+        turn_hidden(last, 1)
+        spread_norms(last)
+        row_squares(a - 1, 0)
+        row_squares(a - 1, 1)
+        invert_sums(a)
+        share_norms(last)
+        scale_weight(a, 1)
+        group_hidden(last, 0)
+        group_hidden(last, 1)
+        unit_rows(a - 1, 0)
+        unit_rows(a - 1, 1)
+        store(a - 1)
+        for c in range(PASSES):
+            quantise_weight(a, c)
+        quantise_hidden(last)
+        scale_weight(last, 0)
+        scale_weight(last, 1)
+        for c in range(PASSES):
+            project(a, c)
+        if W3:
+            idle = hT_psum.tile([P, OUT], F32, name="hT")
+            keep_warm(last, idle, W3)
+        row_squares(a, 0)
+        row_squares(a, 1)
+        invert_sums(last)
+        unit_rows(a, 0)
+        unit_rows(a, 1)
+        store(a)
         for c in range(PASSES):
             quantise_weight(last, c)
             project(last, c)
-        for i in range(B_TILES):
-            row_squares(last, i)
+        row_squares(last, 0)
+        row_squares(last, 1)
         invert_sums(TOKENS)
         for i in range(B_TILES):
             unit_rows(last, i)

@@ -20,15 +20,12 @@ HALVES = 2
 B_TILES = BATCH // P
 J_BLOCKS = OUT // P
 EPS = 1e-12
-GRAM_FROM = [0, 2]
-VECTOR_COLS = [304]*6+[320,352]
+LAST = TOKENS - 1
+EARLY_GRAM = {0: (0, 1, 2, 3), 1: (2, 3)}
+VECTOR_COLS, LATE_VECTOR_COLS = 336, 368
 RUN = 4
+FILL, TAIL_FILL = 2, 8
 
-SCALAR_UNIT = [(l, 0) for l in range(8)] + [(5, 1), (6, 1)]
-SCALAR_HIDDEN = []
-SCALAR_SHARE = [0, 7]
-W1, W2, W3 = 0, 0, 8
-SW = 2
 FLOPS = 2 * BATCH * TOKENS * HIDDEN * OUT
 
 
@@ -77,10 +74,8 @@ def tile_npertokenswishglu_basis_pb_kernel(tc, h, w_down_mix, out):
             load_weight(l, PASSES if l == 0 else 1)
             load_hidden(l)
 
-        warm = hT_psum.tile([P, OUT], F32, name="hT")
-        for n in range(3):
-            nc.tensor.matmul(out=warm[:, :P], lhsT=ident_f32[:], rhs=ident_f32[:], start=True, stop=True)
         wT = {}
+        gram = {}
         col_sq = {}
         col_inv = {}
         inv_rows = {}
@@ -88,30 +83,46 @@ def tile_npertokenswishglu_basis_pb_kernel(tc, h, w_down_mix, out):
         nd = {}
         w_codes = {}
         w_scales = {}
-        grouped = {}
         hT = {}
+        grouped = {}
         h_codes = {}
         h_scales = {}
         y = {}
         row_sq = {}
         row_inv = {}
         unit = {}
-        gram = {}
+        excess = {}
 
-        def clamp(sum_sq, name):
-            excess = small.tile([P, sum_sq.shape[1]], F32, name=name + "_excess")
-            nc.scalar.activation(out=excess[:], in_=sum_sq[:], func=ACT.Relu, bias=-EPS * EPS)
-            return excess
+        def first_products():
+            bank = hT_psum.tile([P, OUT], F32, name="hT")
+            for n in range(3):
+                nc.tensor.matmul(out=bank[:, :P], lhsT=ident_f32[:], rhs=ident_f32[:], start=True, stop=True)
 
-        def invert(excess, name):
-            inv = small.tile([P, excess.shape[1]], F32, name=name + "_inv")
-            nc.scalar.activation(out=inv[:], in_=excess[:], func=ACT.Abs_reciprocal_sqrt, bias=EPS * EPS)
+        def fill(bank, l, passes):
+            for n in range(passes):
+                nc.tensor.matmul_mx(
+                    out=bank[:],
+                    lhsT=h_codes[l][:, :P].bitcast(FP8X4),
+                    lhsT_scale=h_scales[l][:, :P],
+                    rhs=h_codes[l][:].bitcast(FP8X4),
+                    rhs_scale=h_scales[l][:],
+                    start=True,
+                    stop=True,
+                )
+
+        def clamp(sums):
+            over = small.tile([P, sums.shape[1]], F32, name="over%d" % sums.shape[1])
+            nc.scalar.activation(out=over[:], in_=sums, func=ACT.Relu, bias=-EPS * EPS)
+            return over
+
+        def invert(over, name):
+            inv = small.tile([P, over.shape[1]], F32, name=name)
+            nc.scalar.activation(out=inv[:], in_=over[:], func=ACT.Abs_reciprocal_sqrt, bias=EPS * EPS)
             return inv
 
-        def turn_weight(l, m, passes=range(PASSES)):
-            if passes[0] == 0:
-                wT[l, m] = wT_psum.tile([P, ROWS, P], BF16, name="wT")
-            for r in range(passes[0] * PACK, (passes[-1] + 1) * PACK):
+        def turn_weight(l, m):
+            wT[l, m] = wT_psum.tile([P, ROWS, P], BF16, name="wT")
+            for r in range(ROWS):
                 nc.tensor.transpose(wT[l, m][:, r, :], w_sb[l][:, r, m * P : (m + 1) * P], ident_bf[:])
 
         def column_squares(l, m):
@@ -124,7 +135,7 @@ def tile_npertokenswishglu_basis_pb_kernel(tc, h, w_down_mix, out):
             )
 
         def gram_products(l, m, c):
-            if c == 0 and l == 0 and m >= 2:
+            if c == 0 and len(EARLY_GRAM[l]) > 2 and m >= 2:
                 gram[l, m] = wT_psum.tile([P, OUT], F32, name="wT")
             elif c == 0:
                 gram[l, m] = y_psum.tile([P, OUT], F32, name="y")
@@ -147,20 +158,11 @@ def tile_npertokenswishglu_basis_pb_kernel(tc, h, w_down_mix, out):
             )
 
         def vector_cols(l):
-            return VECTOR_COLS[min(l, len(VECTOR_COLS) - 1)]
+            return LATE_VECTOR_COLS if l >= LAST - 1 else VECTOR_COLS
 
-        def spread_norms(l, blocks=range(J_BLOCKS)):
-            bank = wT_psum.tile([P, OUT], F32, name="wT") if blocks[0] or l == TOKENS - 1 else inv_psum.tile([P, OUT], F32, name="inv_rows")
-            for n in range(SW if l >= 2 else 0):
-                nc.tensor.matmul_mx(
-                    out=bank[:],
-                    lhsT=h_codes[l - 1][:, :P].bitcast(FP8X4),
-                    lhsT_scale=h_scales[l - 1][:, :P],
-                    rhs=h_codes[l - 1][:].bitcast(FP8X4),
-                    rhs_scale=h_scales[l - 1][:],
-                    start=True,
-                    stop=True,
-                )
+        def spread_norms(l, bank, blocks, filling):
+            if filling:
+                fill(bank, l - 1, FILL)
             for m in blocks:
                 inv_rows[l, m] = bank
                 nc.tensor.transpose(
@@ -169,23 +171,12 @@ def tile_npertokenswishglu_basis_pb_kernel(tc, h, w_down_mix, out):
                     ident_f32[:],
                 )
 
-        def share_norms(l):
+        def share_norms(l, copy):
             first = vector_cols(l)
             inv_gpsimd[l] = work.tile([P, OUT - first], F32, name="inv_gpsimd")
-            copy = nc.scalar.copy if l in SCALAR_SHARE else nc.vector.tensor_copy
             copy(out=inv_gpsimd[l][:], in_=inv_rows[l, J_BLOCKS - 1][:, first:])
 
-        def scale_columns(engine, l, c, first, last, inv):
-            engine.tensor_tensor(
-                out=nd[l][:, c, first:last, :].rearrange("p (n i) t -> p n t i", i=RUN),
-                in0=w_sb[l][:, c * PACK : (c + 1) * PACK, first:last].rearrange("p t (n i) -> p n t i", i=RUN),
-                in1=inv.rearrange("p (n i) -> p n i", i=RUN)
-                .unsqueeze(2)
-                .to_broadcast([P, (last - first) // RUN, PACK, RUN]),
-                op=ALU.mult,
-            )
-
-        def scale_weight(l, c):
+        def scale_on_gpsimd(l, c):
             if c == 0:
                 nd[l] = work.tile([P, PASSES, OUT, PACK], BF16, name="nd", align_bytes=64)
             first = vector_cols(l)
@@ -195,8 +186,19 @@ def tile_npertokenswishglu_basis_pb_kernel(tc, h, w_down_mix, out):
                 in1=inv_gpsimd[l][:].unsqueeze(2).to_broadcast([P, OUT - first, PACK]),
                 op=ALU.mult,
             )
-            if l > 0:
-                scale_columns(nc.vector, l, c, 0, first, inv_rows[l, 0][:, :first])
+
+        def scale_on_vector(l, c, first, last):
+            inv = inv_rows[l, first // P][:, first:last].rearrange("p (n i) -> p n i", i=RUN)
+            nc.vector.tensor_tensor(
+                out=nd[l][:, c, first:last, :].rearrange("p (n i) t -> p n t i", i=RUN),
+                in0=w_sb[l][:, c * PACK : (c + 1) * PACK, first:last].rearrange("p t (n i) -> p n t i", i=RUN),
+                in1=inv.unsqueeze(2).to_broadcast([P, (last - first) // RUN, PACK, RUN]),
+                op=ALU.mult,
+            )
+
+        def scale_weight(l, c):
+            scale_on_gpsimd(l, c)
+            scale_on_vector(l, c, 0, vector_cols(l))
 
         def quantise_weight(l, c):
             if c == 0:
@@ -222,8 +224,7 @@ def tile_npertokenswishglu_basis_pb_kernel(tc, h, w_down_mix, out):
             if c == 0:
                 grouped[l] = work.tile([P, PASSES * BATCH * PACK], BF16, name="h_grouped", align_bytes=64)
             words = grouped[l][:].bitcast(F32).rearrange("p (c b u) -> p c b u", c=PASSES, u=HALVES)
-            copy = nc.scalar.copy if l in SCALAR_HIDDEN else nc.vector.tensor_copy
-            copy(out=words[:, c], in_=hT[l, c][:].rearrange("p u i b -> p (i b) u"))
+            nc.vector.tensor_copy(out=words[:, c], in_=hT[l, c][:].rearrange("p u i b -> p (i b) u"))
 
         def quantise_hidden(l):
             h_codes[l] = work.tile([P, PASSES * BATCH], U32, name="h_codes", align_bytes=64)
@@ -232,7 +233,7 @@ def tile_npertokenswishglu_basis_pb_kernel(tc, h, w_down_mix, out):
 
         def project(l, c):
             for i in range(B_TILES):
-                if c == 0 and l >= 6:
+                if c == 0 and l >= LAST - 1:
                     y[l, i] = wT_psum.tile([P, OUT], F32, name="wT")
                 elif c == 0:
                     y[l, i] = y_psum.tile([P, OUT], F32, name="y")
@@ -247,213 +248,178 @@ def tile_npertokenswishglu_basis_pb_kernel(tc, h, w_down_mix, out):
                     stop=(c == PASSES - 1),
                 )
 
-        def keep_warm(l, bank, passes):
-            for n in range(passes):
-                nc.tensor.matmul_mx(
-                    out=bank[:],
-                    lhsT=h_codes[l][:, :P].bitcast(FP8X4),
-                    lhsT_scale=h_scales[l][:, :P],
-                    rhs=h_codes[l][:].bitcast(FP8X4),
-                    rhs_scale=h_scales[l][:],
-                    start=True,
-                    stop=True,
-                )
-
-        def row_squares(l, i):
-            y_squares = unread.tile([P, OUT], BF16, name="y_squares")
-            nc.scalar.activation(
-                out=y_squares[:], in_=y[l, i][:], func=ACT.Square, accum_out=row_sq[l][:, i : i + 1]
-            )
-
-        def unit_rows(l, i):
-            if i == 0:
-                unit[l] = result.tile([P, B_TILES, OUT], F32, name="unit")
-            if (l, i) in SCALAR_UNIT:
+        def row_squares(l):
+            for i in range(B_TILES):
+                y_squares = unread.tile([P, OUT], BF16, name="y_squares")
                 nc.scalar.activation(
-                    out=unit[l][:, i, :], in_=y[l, i][:], func=ACT.Copy, scale=row_inv[l][:, i : i + 1]
-                )
-            else:
-                nc.vector.tensor_scalar_mul(
-                    out=unit[l][:, i, :], in0=y[l, i][:], scalar1=row_inv[l][:, i : i + 1]
+                    out=y_squares[:], in_=y[l, i][:], func=ACT.Square, accum_out=row_sq[l][:, i : i + 1]
                 )
 
-        def store_half(l, i):
-            nc.sync.dma_start(out=out.rearrange("(i p) l j -> p i l j", p=P)[:, i, l, :], in_=unit[l][:, i, :])
+        def unit_rows(l):
+            unit[l] = result.tile([P, B_TILES, OUT], F32, name="unit")
+            for i in range(B_TILES):
+                inv = row_inv[l][:, i : i + 1]
+                if (l > 0 and i == 0) or 4 <= l < LAST:
+                    nc.scalar.activation(out=unit[l][:, i, :], in_=y[l, i][:], func=ACT.Copy, scale=inv)
+                else:
+                    nc.vector.tensor_scalar_mul(out=unit[l][:, i, :], in0=y[l, i][:], scalar1=inv)
+
+        out_view = out.rearrange("(i p) l j -> p i l j", p=P)
 
         def store(l):
-            nc.sync.dma_start(out=out.rearrange("(i p) l j -> p i l j", p=P)[:, :, l, :], in_=unit[l][:])
+            nc.sync.dma_start(out=out_view[:, :, l, :], in_=unit[l][:])
 
-        blocks = [(l, m) for l in range(1, TOKENS) for m in range(2 if l < len(GRAM_FROM) else J_BLOCKS)]
-        sums = {}
-        last = TOKENS - 1
-        for l in range(-1, TOKENS + 1):
-            columns = J_BLOCKS if l + 1 < last else 0
-            rows = B_TILES if l > 0 else 0
-            sums[l] = small.tile([P, columns + rows], F32, name="sums%d" % l)
-            if columns:
-                col_sq[l + 1] = sums[l][:, :columns]
-            if rows:
-                row_sq[l - 1] = sums[l][:, columns:]
-        col_sq[last] = small.tile([P, J_BLOCKS], F32, name="last_col_sq")
+        to_turn = [(l, m) for l in range(TOKENS) for m in range(J_BLOCKS) if m not in EARLY_GRAM.get(l, ())]
+        to_square = list(to_turn)
 
-        def invert_sums(l):
-            inv = invert(clamp(sums[l], "sums"), "sums")
-            columns = J_BLOCKS if l + 1 < last else 0
-            if columns:
-                col_inv[l + 1] = inv[:, :columns]
-            row_inv[l - 1] = inv[:, columns:]
-
-        to_turn = list(blocks)
-        to_square = list(blocks)
-        col_excess = {}
-        row_excess = {}
-
-        def turn_next():
-            if to_turn:
+        def turn_next(blocks):
+            for n in range(min(blocks, len(to_turn))):
                 turn_weight(*to_turn.pop(0))
 
-        def square_next():
-            if to_square:
+        def square_next(blocks):
+            for n in range(min(blocks, len(to_square))):
                 column_squares(*to_square.pop(0))
 
-        def clamp_columns(l):
-            if l < TOKENS:
-                col_excess[l] = clamp(col_sq[l], "col")
+        step_sums = {}
+        for l in range(-1, TOKENS + 1):
+            columns = J_BLOCKS if l + 1 < LAST else 0
+            rows = B_TILES if l > 0 else 0
+            step_sums[l] = small.tile([P, columns + rows], F32, name="step_sums%d" % (columns + rows))
+            if columns:
+                col_sq[l + 1] = step_sums[l][:, :columns]
+            if rows:
+                row_sq[l - 1] = step_sums[l][:, columns:]
+        col_sq[LAST] = small.tile([P, J_BLOCKS], F32, name="last_col_sq")
 
-        def invert_columns(l):
-            if l < TOKENS:
-                col_inv[l] = invert(col_excess[l], "col")
+        def clamp_step(l):
+            excess[l] = clamp(step_sums[l][:])
 
+        def invert_step(l):
+            inv = invert(excess[l], "inv_step%d" % excess[l].shape[1])
+            columns = J_BLOCKS if l + 1 < LAST else 0
+            if columns:
+                col_inv[l + 1] = inv[:, :columns]
+            if l > 0:
+                row_inv[l - 1] = inv[:, columns:]
+
+        first_products()
         for c in range(PASSES):
-            for m in range(J_BLOCKS):
+            for m in EARLY_GRAM[0]:
                 gram_products(0, m, c)
-        for m in range(J_BLOCKS):
+        for m in EARLY_GRAM[0]:
             gram_diagonal(0, m)
-        HALF = J_BLOCKS // 2
+        half = OUT // 2
         col_inv[0] = small.tile([P, J_BLOCKS], F32, name="col_inv0")
-        def inv_half(k):
-            cols = slice(k * HALF, (k + 1) * HALF)
-            ex = small.tile([P, HALF], F32, name="exh")
-            nc.scalar.activation(out=ex[:], in_=sums[-1][:, cols], func=ACT.Relu, bias=-EPS * EPS)
-            nc.scalar.activation(out=col_inv[0][:, cols], in_=ex[:], func=ACT.Abs_reciprocal_sqrt, bias=EPS * EPS)
-        inv_half(0)
-        turn_hidden(0, 0)
-        spread_norms(0, range(HALF))
-        inv_half(1)
-        spread_norms(0, range(HALF, J_BLOCKS))
-        share_norms(0)
+        half_blocks = [range(0, J_BLOCKS // 2), range(J_BLOCKS // 2, J_BLOCKS)]
+        half_banks = [
+            inv_psum.tile([P, OUT], F32, name="inv_rows"),
+            wT_psum.tile([P, OUT], F32, name="wT"),
+        ]
+        for k in range(2):
+            cols = slice(half_blocks[k].start, half_blocks[k].stop)
+            over = clamp(col_sq[0][:, cols])
+            nc.scalar.activation(
+                out=col_inv[0][:, cols], in_=over[:], func=ACT.Abs_reciprocal_sqrt, bias=EPS * EPS
+            )
+            if k == 0:
+                turn_hidden(0, 0)
+            spread_norms(0, half_banks[k], half_blocks[k], False)
+        share_norms(0, nc.scalar.copy)
         group_hidden(0, 0)
         turn_hidden(0, 1)
-        scale_weight(0, 0)
-        scale_weight(0, 1)
-        mid = HALF * P
         for c in range(PASSES):
-            scale_columns(nc.vector, 0, c, 0, mid, inv_rows[0, 0][:, :mid])
-        if vector_cols(0) > mid:
+            scale_on_gpsimd(0, c)
+        for first, last in ((0, half), (half, VECTOR_COLS)):
             for c in range(PASSES):
-                scale_columns(nc.vector, 0, c, mid, vector_cols(0), inv_rows[0, HALF][:, mid:vector_cols(0)])
+                scale_on_vector(0, c, first, last)
         group_hidden(0, 1)
-        turn_next()
-        turn_next()
-        square_next()
-        square_next()
-        for m in range(2, J_BLOCKS):
-            gram_products(1, m, 0)
-            gram_products(1, m, 1)
-        turn_hidden(1, 0)
-        turn_hidden(1, 1)
-        gram_diagonal(1, 2)
-        gram_diagonal(1, 3)
-        invert_sums(0)
+        turn_next(2)
+        square_next(2)
+        for m in EARLY_GRAM[1]:
+            for c in range(PASSES):
+                gram_products(1, m, c)
+        for c in range(PASSES):
+            turn_hidden(1, c)
+        for m in EARLY_GRAM[1]:
+            gram_diagonal(1, m)
+        clamp_step(0)
+        invert_step(0)
         group_hidden(1, 0)
-        turn_next()
-        spread_norms(1)
+        turn_next(1)
+        spread_norms(1, inv_psum.tile([P, OUT], F32, name="inv_rows"), range(J_BLOCKS), False)
         group_hidden(1, 1)
         quantise_hidden(0)
-        square_next()
-        turn_next()
-        square_next()
-        turn_next()
-        square_next()
-        turn_next()
-        square_next()
-        turn_next()
+        for n in range(4):
+            square_next(1)
+            turn_next(1)
         for c in range(PASSES):
             quantise_weight(0, c)
         quantise_hidden(1)
-        for l in range(1, last - 1):
-            share_norms(l)
-            scale_weight(l, 0)
+
+        for l in range(1, LAST - 1):
+            share_norms(l, nc.vector.tensor_copy)
+            for c in range(PASSES):
+                scale_weight(l, c)
             for c in range(PASSES):
                 project(l - 1, c)
-            turn_hidden(l + 1, 0)
-            turn_hidden(l + 1, 1)
-            turn_next()
-            row_squares(l - 1, 0)
-            row_squares(l - 1, 1)
-            invert_sums(l)
-            square_next()
-            scale_weight(l, 1)
-            spread_norms(l + 1)
-            group_hidden(l + 1, 0)
-            group_hidden(l + 1, 1)
-            turn_next()
-            square_next()
-            turn_next()
-            unit_rows(l - 1, 0)
-            unit_rows(l - 1, 1)
-            store(l - 1)
-            square_next()
-            turn_next()
-            square_next()
+            for c in range(PASSES):
+                turn_hidden(l + 1, c)
+                group_hidden(l + 1, c)
             for c in range(PASSES):
                 quantise_weight(l, c)
+            turn_next(2)
+            row_squares(l - 1)
+            clamp_step(l)
+            square_next(1)
+            invert_step(l)
+            spread_norms(l + 1, inv_psum.tile([P, OUT], F32, name="inv_rows"), range(J_BLOCKS), True)
+            turn_next(1)
+            square_next(1)
+            turn_next(1)
+            unit_rows(l - 1)
+            store(l - 1)
             quantise_hidden(l + 1)
-        while to_turn:
-            turn_next()
-        while to_square:
-            square_next()
-        col_inv[last] = invert(clamp(col_sq[last], "col"), "col")
-        a = last - 1
-        share_norms(a)
-        scale_weight(a, 0)
+            square_next(2)
+
+        turn_next(len(to_turn))
+        square_next(len(to_square))
+        col_inv[LAST] = invert(clamp(col_sq[LAST][:]), "last_col_inv")
+        l = LAST - 1
+        share_norms(l, nc.vector.tensor_copy)
+        scale_weight(l, 0)
         for c in range(PASSES):
-            project(a - 1, c)
-        turn_hidden(last, 0)
-        turn_hidden(last, 1)
-        spread_norms(last)
-        row_squares(a - 1, 0)
-        row_squares(a - 1, 1)
-        invert_sums(a)
-        share_norms(last)
-        scale_weight(a, 1)
-        group_hidden(last, 0)
-        group_hidden(last, 1)
-        unit_rows(a - 1, 0)
-        unit_rows(a - 1, 1)
-        store(a - 1)
+            project(l - 1, c)
         for c in range(PASSES):
-            quantise_weight(a, c)
-        quantise_hidden(last)
-        scale_weight(last, 0)
-        scale_weight(last, 1)
+            turn_hidden(LAST, c)
+        spread_norms(LAST, wT_psum.tile([P, OUT], F32, name="wT"), range(J_BLOCKS), True)
+        row_squares(l - 1)
+        clamp_step(l)
+        invert_step(l)
+        share_norms(LAST, nc.scalar.copy)
+        scale_weight(l, 1)
         for c in range(PASSES):
-            project(a, c)
-        if W3:
-            idle = hT_psum.tile([P, OUT], F32, name="hT")
-            keep_warm(last, idle, W3)
-        row_squares(a, 0)
-        row_squares(a, 1)
-        invert_sums(last)
-        unit_rows(a, 0)
-        unit_rows(a, 1)
-        store(a)
+            group_hidden(LAST, c)
+        unit_rows(l - 1)
+        store(l - 1)
         for c in range(PASSES):
-            quantise_weight(last, c)
-            project(last, c)
-        row_squares(last, 0)
-        row_squares(last, 1)
-        invert_sums(TOKENS)
+            quantise_weight(l, c)
+        quantise_hidden(LAST)
+        for c in range(PASSES):
+            scale_weight(LAST, c)
+        for c in range(PASSES):
+            project(l, c)
+        fill(hT_psum.tile([P, OUT], F32, name="hT"), LAST, TAIL_FILL)
+        row_squares(l)
+        clamp_step(LAST)
+        invert_step(LAST)
+        unit_rows(l)
+        store(l)
+        for c in range(PASSES):
+            quantise_weight(LAST, c)
+            project(LAST, c)
+        row_squares(LAST)
+        clamp_step(TOKENS)
+        invert_step(TOKENS)
+        unit_rows(LAST)
         for i in range(B_TILES):
-            unit_rows(last, i)
-            store_half(last, i)
+            nc.sync.dma_start(out=out_view[:, i, LAST, :], in_=unit[LAST][:, i, :])

from contextlib import ExitStack

import concourse.mybir as mybir
from concourse.masks import make_identity

BF16 = mybir.dt.bfloat16
F32 = mybir.dt.float32
U32 = mybir.dt.uint32
U8 = mybir.dt.uint8
FP8X4 = mybir.dt.float8_e4m3fn_x4
ACT = mybir.ActivationFunctionType
ALU = mybir.AluOpType

P = 128
PACK = 4
BATCH, TOKENS, HIDDEN, OUT = 256, 8, 1024, 512
PASSES = HIDDEN // (P * PACK)
ROWS = PASSES * PACK
HALVES = 2
B_TILES = BATCH // P
J_BLOCKS = OUT // P
EPS = 1e-12
LAST = TOKENS - 1
EARLY_GRAM = {0: (0, 1, 2, 3), 1: (2, 3)}
VECTOR_COLS, LATE_VECTOR_COLS = 336, 368
RUN = 4
FILL, TAIL_FILL = 2, 8

FLOPS = 2 * BATCH * TOKENS * HIDDEN * OUT


def tile_npertokenswishglu_basis_pb_kernel(tc, h, w_down_mix, out):
    nc = tc.nc
    with ExitStack() as stack:
        const = stack.enter_context(tc.tile_pool(name="const", bufs=1))
        w_pool = stack.enter_context(tc.tile_pool(name="w_pool", bufs=TOKENS))
        h_pool = stack.enter_context(tc.tile_pool(name="h_pool", bufs=TOKENS))
        work = stack.enter_context(tc.tile_pool(name="work", bufs=2))
        unread = stack.enter_context(tc.tile_pool(name="unread", bufs=2))
        small = stack.enter_context(tc.tile_pool(name="small", bufs=TOKENS))
        result = stack.enter_context(tc.tile_pool(name="result", bufs=3))
        wT_psum = stack.enter_context(tc.psum_pool(name="wT_psum", bufs=3))
        inv_psum = stack.enter_context(tc.psum_pool(name="inv_psum", bufs=1))
        hT_psum = stack.enter_context(tc.psum_pool(name="hT_psum", bufs=2))
        y_psum = stack.enter_context(tc.psum_pool(name="y_psum", bufs=2))
        stack.enter_context(tc.manual_schedule())

        ident_f32 = const.tile([P, P], F32, name="ident_f32")
        make_identity(nc, ident_f32[:])
        ident_bf = const.tile([P, P], BF16, name="ident_bf")
        make_identity(nc, ident_bf[:])

        one = const.tile([P, 1], F32, name="one")
        nc.vector.memset(one[:], 1.0)
        nc.scalar.activation(out=one[:], in_=one[:], func=ACT.Abs_reciprocal_sqrt)

        w_sb = {}
        h_sb = {}
        h_view = h.rearrange("(i p) l f -> p i l f", p=P)

        def load_weight(l, loads):
            w_sb[l] = w_pool.tile([P, ROWS, OUT], BF16, name="w_tile")
            w_out = w_sb[l][:].rearrange("p (c t) j -> p c (t j)", t=PACK)
            w_in = w_down_mix[l].rearrange("(c p t) j -> p c (t j)", p=P, t=PACK)
            step = PASSES // loads
            for c in range(0, PASSES, step):
                nc.sync.dma_start(out=w_out[:, c : c + step], in_=w_in[:, c : c + step])

        def load_hidden(l):
            h_sb[l] = h_pool.tile([P, B_TILES, HIDDEN], BF16, name="h_tile")
            nc.sync.dma_start(out=h_sb[l][:], in_=h_view[:, :, l, :])

        for l in range(TOKENS):
            load_weight(l, PASSES if l == 0 else 1)
            load_hidden(l)

        wT = {}
        gram = {}
        col_sq = {}
        col_inv = {}
        inv_rows = {}
        inv_gpsimd = {}
        nd = {}
        w_codes = {}
        w_scales = {}
        hT = {}
        grouped = {}
        h_codes = {}
        h_scales = {}
        y = {}
        row_sq = {}
        row_inv = {}
        unit = {}
        excess = {}

        def first_products():
            bank = hT_psum.tile([P, OUT], F32, name="hT")
            for n in range(3):
                nc.tensor.matmul(out=bank[:, :P], lhsT=ident_f32[:], rhs=ident_f32[:], start=True, stop=True)

        def fill(bank, l, passes):
            for n in range(passes):
                nc.tensor.matmul_mx(
                    out=bank[:],
                    lhsT=h_codes[l][:, :P].bitcast(FP8X4),
                    lhsT_scale=h_scales[l][:, :P],
                    rhs=h_codes[l][:].bitcast(FP8X4),
                    rhs_scale=h_scales[l][:],
                    start=True,
                    stop=True,
                )

        def clamp(sums):
            over = small.tile([P, sums.shape[1]], F32, name="over%d" % sums.shape[1])
            nc.scalar.activation(out=over[:], in_=sums, func=ACT.Relu, bias=-EPS * EPS)
            return over

        def invert(over, name):
            inv = small.tile([P, over.shape[1]], F32, name=name)
            nc.scalar.activation(out=inv[:], in_=over[:], func=ACT.Abs_reciprocal_sqrt, bias=EPS * EPS)
            return inv

        def turn_weight(l, m):
            wT[l, m] = wT_psum.tile([P, ROWS, P], BF16, name="wT")
            for r in range(ROWS):
                nc.tensor.transpose(wT[l, m][:, r, :], w_sb[l][:, r, m * P : (m + 1) * P], ident_bf[:])

        def column_squares(l, m):
            squares = unread.tile([P, ROWS * P], BF16, name="squares")
            nc.scalar.activation(
                out=squares[:],
                in_=wT[l, m][:].rearrange("p r f -> p (r f)"),
                func=ACT.Square,
                accum_out=col_sq[l][:, m : m + 1],
            )

        def gram_products(l, m, c):
            if c == 0 and len(EARLY_GRAM[l]) > 2 and m >= 2:
                gram[l, m] = wT_psum.tile([P, OUT], F32, name="wT")
            elif c == 0:
                gram[l, m] = y_psum.tile([P, OUT], F32, name="y")
            for r in range(c * PACK, (c + 1) * PACK):
                block = w_sb[l][:, r, m * P : (m + 1) * P]
                nc.tensor.matmul(
                    out=gram[l, m][:, :P], lhsT=block, rhs=block, start=(r == 0), stop=(r == ROWS - 1)
                )

        def gram_diagonal(l, m):
            diagonal = unread.tile([P, P], F32, name="diagonal")
            nc.vector.scalar_tensor_tensor(
                out=diagonal[:],
                in0=gram[l, m][:, :P],
                scalar=1.0,
                in1=ident_f32[:],
                op0=ALU.mult,
                op1=ALU.mult,
                accum_out=col_sq[l][:, m : m + 1],
            )

        def vector_cols(l):
            return LATE_VECTOR_COLS if l >= LAST - 1 else VECTOR_COLS

        def spread_norms(l, bank, blocks, filling):
            if filling:
                fill(bank, l - 1, FILL)
            for m in blocks:
                inv_rows[l, m] = bank
                nc.tensor.transpose(
                    bank[:, m * P : (m + 1) * P],
                    col_inv[l][:, m : m + 1].to_broadcast([P, P]),
                    ident_f32[:],
                )

        def share_norms(l, copy):
            first = vector_cols(l)
            inv_gpsimd[l] = work.tile([P, OUT - first], F32, name="inv_gpsimd")
            copy(out=inv_gpsimd[l][:], in_=inv_rows[l, J_BLOCKS - 1][:, first:])

        def scale_on_gpsimd(l, c):
            if c == 0:
                nd[l] = work.tile([P, PASSES, OUT, PACK], BF16, name="nd", align_bytes=64)
            first = vector_cols(l)
            nc.gpsimd.tensor_tensor(
                out=nd[l][:, c, first:, :],
                in0=w_sb[l][:, c * PACK : (c + 1) * PACK, first:].rearrange("p t j -> p j t"),
                in1=inv_gpsimd[l][:].unsqueeze(2).to_broadcast([P, OUT - first, PACK]),
                op=ALU.mult,
            )

        def scale_on_vector(l, c, first, last):
            inv = inv_rows[l, first // P][:, first:last].rearrange("p (n i) -> p n i", i=RUN)
            nc.vector.tensor_tensor(
                out=nd[l][:, c, first:last, :].rearrange("p (n i) t -> p n t i", i=RUN),
                in0=w_sb[l][:, c * PACK : (c + 1) * PACK, first:last].rearrange("p t (n i) -> p n t i", i=RUN),
                in1=inv.unsqueeze(2).to_broadcast([P, (last - first) // RUN, PACK, RUN]),
                op=ALU.mult,
            )

        def scale_weight(l, c):
            scale_on_gpsimd(l, c)
            scale_on_vector(l, c, 0, vector_cols(l))

        def quantise_weight(l, c):
            if c == 0:
                w_codes[l] = work.tile([P, PASSES, OUT], U32, name="w_codes", align_bytes=64)
                w_scales[l] = work.tile([P, PASSES, OUT], U8, name="w_scales", align_bytes=64)
            nc.vector.quantize_mx(
                out=w_codes[l][:, c, :].bitcast(FP8X4),
                scales=w_scales[l][:, c, :],
                in_=nd[l][:, c].rearrange("p j t -> p (j t)"),
            )

        def turn_hidden(l, c):
            hT[l, c] = hT_psum.tile([P, HALVES, B_TILES, P], F32, name="hT")
            for u in range(HALVES):
                for i in range(B_TILES):
                    words = h_sb[l][:, i, :].bitcast(F32)
                    first = c * HALVES * P
                    nc.tensor.transpose(
                        hT[l, c][:, u, i, :], words[:, first + u : first + HALVES * P : HALVES], ident_f32[:]
                    )

        def group_hidden(l, c):
            if c == 0:
                grouped[l] = work.tile([P, PASSES * BATCH * PACK], BF16, name="h_grouped", align_bytes=64)
            words = grouped[l][:].bitcast(F32).rearrange("p (c b u) -> p c b u", c=PASSES, u=HALVES)
            nc.vector.tensor_copy(out=words[:, c], in_=hT[l, c][:].rearrange("p u i b -> p (i b) u"))

        def quantise_hidden(l):
            h_codes[l] = work.tile([P, PASSES * BATCH], U32, name="h_codes", align_bytes=64)
            h_scales[l] = work.tile([P, PASSES * BATCH], U8, name="h_scales", align_bytes=64)
            nc.vector.quantize_mx(out=h_codes[l][:].bitcast(FP8X4), scales=h_scales[l][:], in_=grouped[l][:])

        def project(l, c):
            for i in range(B_TILES):
                if c == 0 and l >= LAST - 1:
                    y[l, i] = wT_psum.tile([P, OUT], F32, name="wT")
                elif c == 0:
                    y[l, i] = y_psum.tile([P, OUT], F32, name="y")
                b_cols = slice((c * B_TILES + i) * P, (c * B_TILES + i + 1) * P)
                nc.tensor.matmul_mx(
                    out=y[l, i][:],
                    lhsT=h_codes[l][:, b_cols].bitcast(FP8X4),
                    lhsT_scale=h_scales[l][:, b_cols],
                    rhs=w_codes[l][:, c, :].bitcast(FP8X4),
                    rhs_scale=w_scales[l][:, c, :],
                    start=(c == 0),
                    stop=(c == PASSES - 1),
                )

        def row_squares(l):
            for i in range(B_TILES):
                y_squares = unread.tile([P, OUT], BF16, name="y_squares")
                nc.scalar.activation(
                    out=y_squares[:], in_=y[l, i][:], func=ACT.Square, accum_out=row_sq[l][:, i : i + 1]
                )

        def unit_rows(l):
            unit[l] = result.tile([P, B_TILES, OUT], F32, name="unit")
            for i in range(B_TILES):
                inv = row_inv[l][:, i : i + 1]
                if (l > 0 and i == 0) or 4 <= l < LAST:
                    nc.scalar.activation(out=unit[l][:, i, :], in_=y[l, i][:], func=ACT.Copy, scale=inv)
                else:
                    nc.vector.tensor_scalar_mul(out=unit[l][:, i, :], in0=y[l, i][:], scalar1=inv)

        out_view = out.rearrange("(i p) l j -> p i l j", p=P)

        def store(l):
            nc.sync.dma_start(out=out_view[:, :, l, :], in_=unit[l][:])

        to_turn = [(l, m) for l in range(TOKENS) for m in range(J_BLOCKS) if m not in EARLY_GRAM.get(l, ())]
        to_square = list(to_turn)

        def turn_next(blocks):
            for n in range(min(blocks, len(to_turn))):
                turn_weight(*to_turn.pop(0))

        def square_next(blocks):
            for n in range(min(blocks, len(to_square))):
                column_squares(*to_square.pop(0))

        step_sums = {}
        for l in range(-1, TOKENS + 1):
            columns = J_BLOCKS if l + 1 < LAST else 0
            rows = B_TILES if l > 0 else 0
            step_sums[l] = small.tile([P, columns + rows], F32, name="step_sums%d" % (columns + rows))
            if columns:
                col_sq[l + 1] = step_sums[l][:, :columns]
            if rows:
                row_sq[l - 1] = step_sums[l][:, columns:]
        col_sq[LAST] = small.tile([P, J_BLOCKS], F32, name="last_col_sq")

        def clamp_step(l):
            excess[l] = clamp(step_sums[l][:])

        def invert_step(l):
            inv = invert(excess[l], "inv_step%d" % excess[l].shape[1])
            columns = J_BLOCKS if l + 1 < LAST else 0
            if columns:
                col_inv[l + 1] = inv[:, :columns]
            if l > 0:
                row_inv[l - 1] = inv[:, columns:]

        first_products()
        for c in range(PASSES):
            for m in EARLY_GRAM[0]:
                gram_products(0, m, c)
        for m in EARLY_GRAM[0]:
            gram_diagonal(0, m)
        half = OUT // 2
        col_inv[0] = small.tile([P, J_BLOCKS], F32, name="col_inv0")
        half_blocks = [range(0, J_BLOCKS // 2), range(J_BLOCKS // 2, J_BLOCKS)]
        half_banks = [
            inv_psum.tile([P, OUT], F32, name="inv_rows"),
            wT_psum.tile([P, OUT], F32, name="wT"),
        ]
        for k in range(2):
            cols = slice(half_blocks[k].start, half_blocks[k].stop)
            over = clamp(col_sq[0][:, cols])
            nc.scalar.activation(
                out=col_inv[0][:, cols], in_=over[:], func=ACT.Abs_reciprocal_sqrt, bias=EPS * EPS
            )
            if k == 0:
                turn_hidden(0, 0)
            spread_norms(0, half_banks[k], half_blocks[k], False)
        share_norms(0, nc.scalar.copy)
        group_hidden(0, 0)
        turn_hidden(0, 1)
        for c in range(PASSES):
            scale_on_gpsimd(0, c)
        for first, last in ((0, half), (half, VECTOR_COLS)):
            for c in range(PASSES):
                scale_on_vector(0, c, first, last)
        group_hidden(0, 1)
        turn_next(2)
        square_next(2)
        for m in EARLY_GRAM[1]:
            for c in range(PASSES):
                gram_products(1, m, c)
        for c in range(PASSES):
            turn_hidden(1, c)
        for m in EARLY_GRAM[1]:
            gram_diagonal(1, m)
        clamp_step(0)
        invert_step(0)
        group_hidden(1, 0)
        turn_next(1)
        spread_norms(1, inv_psum.tile([P, OUT], F32, name="inv_rows"), range(J_BLOCKS), False)
        group_hidden(1, 1)
        quantise_hidden(0)
        for n in range(4):
            square_next(1)
            turn_next(1)
        for c in range(PASSES):
            quantise_weight(0, c)
        quantise_hidden(1)

        for l in range(1, LAST - 1):
            share_norms(l, nc.vector.tensor_copy)
            for c in range(PASSES):
                scale_weight(l, c)
            for c in range(PASSES):
                project(l - 1, c)
            for c in range(PASSES):
                turn_hidden(l + 1, c)
                group_hidden(l + 1, c)
            for c in range(PASSES):
                quantise_weight(l, c)
            turn_next(2)
            row_squares(l - 1)
            clamp_step(l)
            square_next(1)
            invert_step(l)
            spread_norms(l + 1, inv_psum.tile([P, OUT], F32, name="inv_rows"), range(J_BLOCKS), True)
            turn_next(1)
            square_next(1)
            turn_next(1)
            unit_rows(l - 1)
            store(l - 1)
            quantise_hidden(l + 1)
            square_next(2)

        turn_next(len(to_turn))
        square_next(len(to_square))
        col_inv[LAST] = invert(clamp(col_sq[LAST][:]), "last_col_inv")
        l = LAST - 1
        share_norms(l, nc.vector.tensor_copy)
        scale_weight(l, 0)
        for c in range(PASSES):
            project(l - 1, c)
        for c in range(PASSES):
            turn_hidden(LAST, c)
        spread_norms(LAST, wT_psum.tile([P, OUT], F32, name="wT"), range(J_BLOCKS), True)
        row_squares(l - 1)
        clamp_step(l)
        invert_step(l)
        share_norms(LAST, nc.scalar.copy)
        scale_weight(l, 1)
        for c in range(PASSES):
            group_hidden(LAST, c)
        unit_rows(l - 1)
        store(l - 1)
        for c in range(PASSES):
            quantise_weight(l, c)
        quantise_hidden(LAST)
        for c in range(PASSES):
            scale_weight(LAST, c)
        for c in range(PASSES):
            project(l, c)
        fill(hT_psum.tile([P, OUT], F32, name="hT"), LAST, TAIL_FILL)
        row_squares(l)
        clamp_step(LAST)
        invert_step(LAST)
        unit_rows(l)
        store(l)
        for c in range(PASSES):
            quantise_weight(LAST, c)
            project(LAST, c)
        row_squares(LAST)
        clamp_step(TOKENS)
        invert_step(TOKENS)
        unit_rows(LAST)
        for i in range(B_TILES):
            nc.sync.dma_start(out=out_view[:, i, LAST, :], in_=unit[LAST][:, i, :])
